import numpy as np
import ml_dtypes


def mxq(x, axis, fmt="e4m3"):
    dtype, down = {"e4m3": (ml_dtypes.float8_e4m3fn, 7), "e5m2": (ml_dtypes.float8_e5m2, 14)}[fmt]
    v = np.moveaxis(np.asarray(x, np.float32).astype(ml_dtypes.bfloat16).astype(np.float64), axis, -1)
    blocks = v.reshape(v.shape[:-1] + (-1, 32))
    amax = np.abs(blocks).max(-1, keepdims=True)
    byte = np.maximum(np.where(amax > 0, np.frexp(amax)[1] - 1 + 127, 0) - down, 1)
    scale = np.exp2(byte - 127.0)
    codes = (blocks / scale).astype(np.float32).astype(dtype).astype(np.float64)
    return np.moveaxis((codes * scale).reshape(v.shape), -1, axis)


WIDE = False


def mx_kscale(k):
    if not WIDE:
        return np.ones(k)
    levels = np.array([10, -10, 5, -5, 0])
    a = np.random.permutation(np.resize(levels, k // 512 * 4)).reshape(k // 512, 4)
    idx = np.arange(k)
    return np.exp2(a[idx // 512, idx % 128 // 32])


BF16 = ml_dtypes.bfloat16


def bf(x):
    return np.asarray(x, np.float32).astype(BF16)


def f64(x):
    return np.asarray(x).astype(np.float64)


B, H, N, P = 4, 4, 1024, 128
MASK_BIAS = 1.0e9
QS = 1.75 / np.sqrt(P)
KEEP = 0.75


def setup_inputs():
    s = mx_kscale(N)
    up = s.max() / s
    c = np.sqrt(2.0 * np.log(up))
    q = np.random.standard_normal((B, H, N, P)) * QS
    k = np.random.standard_normal((B, H, N, P)) * QS
    k[..., 0] += c
    v = np.random.standard_normal((B, H, N, P)) * 0.25 * up[:, None]
    mask = np.random.random((B, N)) < KEEP
    return {"q_s": bf(q), "k_s": bf(k), "v_s": bf(v), "mask": bf(mask)}


def reference(q_s, k_s, v_s, mask):
    diag_q = 0.5 * np.sum(f64(q_s) * f64(q_s), axis=-1)[..., :, None]
    diag_k = 0.5 * np.sum(f64(k_s) * f64(k_s), axis=-1)[..., None, :]
    product = (f64(q_s) @ f64(k_s).transpose(0, 1, 3, 2)
               - diag_q - diag_k
               - MASK_BIAS * (1.0 - f64(mask))[:, None, None, :])
    attn = np.exp(product)
    return mxq(attn, 3, "e4m3") @ mxq(f64(v_s), 2, "e4m3")

@@ -1,0 +1,235 @@
+from contextlib import ExitStack
+
+import concourse.mybir as mybir
+from concourse.masks import make_identity
+
+BF16 = mybir.dt.bfloat16
+F32 = mybir.dt.float32
+U32 = mybir.dt.uint32
+U8 = mybir.dt.uint8
+FP8X4 = mybir.dt.float8_e4m3fn_x4
+ALU = mybir.AluOpType
+ACT = mybir.ActivationFunctionType
+AXIS = mybir.AxisListType
+
+BATCHES, HEADS, TOKENS, FEATURES = 4, 4, 1024, 128
+P = 128
+PACK = 4
+K_PASS = P * PACK
+PASSES = TOKENS // K_PASS
+TILES = TOKENS // P
+Q_HALF = 512
+HALVES = TOKENS // Q_HALF
+Q_TILES_PER_HALF = Q_HALF // P
+RUN = 4
+MASK_BIAS = 1.0e9
+
+FLOPS = 2 * 2 * BATCHES * HEADS * TOKENS * TOKENS * FEATURES
+
+
+def tile_softmaxattention_kde_pa_t_kernel(tc, q_s, k_s, v_s, mask, out):
+    nc = tc.nc
+    with ExitStack() as ctx:
+        const = ctx.enter_context(tc.tile_pool(name="const", bufs=1))
+        inputs = ctx.enter_context(tc.tile_pool(name="inputs", bufs=3))
+        prep = ctx.enter_context(tc.tile_pool(name="prep", bufs=2))
+        work = ctx.enter_context(tc.tile_pool(name="work", bufs=3))
+        score_banks = ctx.enter_context(tc.psum_pool(name="score_banks", bufs=3))
+        factor_banks = ctx.enter_context(tc.psum_pool(name="factor_banks", bufs=2))
+        out_banks = ctx.enter_context(tc.psum_pool(name="out_banks", bufs=1))
+        turn_banks = ctx.enter_context(tc.psum_pool(name="turn_banks", bufs=2))
+
+        ident_bf16 = const.tile([P, P], BF16)
+        make_identity(nc, ident_bf16[:])
+        ident_f32 = const.tile([P, P], F32)
+        make_identity(nc, ident_f32[:])
+
+        warm = const.tile([P, 1], F32)
+        nc.vector.memset(warm[:], 0.0)
+        nc.scalar.activation(out=warm[:], in_=warm[:], func=ACT.Exp)
+
+        mask_rows = const.tile([P, BATCHES * PASSES, PACK], BF16)
+        with nc.allow_non_contiguous_dma(reason="the mask is 8 KiB, loaded once, 4 keys a run"):
+            nc.sync.dma_start(
+                out=mask_rows[:],
+                in_=mask.rearrange("b (c p t) -> p (b c) t", c=PASSES, t=PACK),
+            )
+        mask_term = const.tile([P, BATCHES * TILES], F32)
+        nc.vector.tensor_scalar(
+            out=mask_term[:],
+            in0=mask_rows[:].rearrange("p a t -> p (a t)"),
+            scalar1=MASK_BIAS,
+            scalar2=-MASK_BIAS,
+            op0=ALU.mult,
+            op1=ALU.add,
+        )
+
+        def load(head):
+            b, h = divmod(head, HEADS)
+            qk = inputs.tile([P, 2, TILES, FEATURES], BF16)
+            nc.sync.dma_start(
+                out=qk[:, 0], in_=q_s[b, h].rearrange("(p j) d -> p j d", j=TILES)
+            )
+            nc.sync.dma_start(
+                out=qk[:, 1].rearrange("p (c t) d -> p c t d", c=PASSES),
+                in_=k_s[b, h].rearrange("(c p t) d -> p c t d", c=PASSES, t=PACK),
+            )
+            v_rows = inputs.tile([P, PASSES, PACK, FEATURES], BF16)
+            nc.sync.dma_start(
+                out=v_rows[:],
+                in_=v_s[b, h].rearrange("(c p t) d -> p c t d", c=PASSES, t=PACK),
+            )
+            return {"qk": qk, "v_rows": v_rows}
+
+        def prepare(head, loaded):
+            b = head // HEADS
+            qk = loaded["qk"]
+
+            turned = []
+            for a in range(2):
+                turned_bank = turn_banks.tile([P, TILES, P], BF16, tag="turn")
+                for j in range(TILES):
+                    nc.tensor.transpose(turned_bank[:, j, :], qk[:, a, j, :], ident_bf16[:])
+                turned_sb = prep.tile([P, TILES, P], BF16, name="turned%d" % a)
+                nc.scalar.copy(out=turned_sb[:], in_=turned_bank[:])
+                turned.append(turned_sb)
+
+            v_grouped = prep.tile([P, PASSES, FEATURES, PACK], BF16, align_bytes=64)
+            nc.vector.tensor_copy(
+                out=v_grouped[:], in_=loaded["v_rows"][:].rearrange("p c t w -> p c w t")
+            )
+            v_codes = prep.tile([P, PASSES, FEATURES], U32, align_bytes=64)
+            v_scales = prep.tile([P, PASSES, FEATURES], U8, align_bytes=64)
+            nc.vector.quantize_mx(
+                out=v_codes[:].rearrange("p c w -> p (c w)").bitcast(FP8X4),
+                scales=v_scales[:].rearrange("p c w -> p (c w)"),
+                in_=v_grouped[:].rearrange("p c w t -> p (c w t)"),
+            )
+            rows = qk[:].rearrange("p a j d -> p (a j) d")
+            squares = prep.tile([P, 2 * TILES, FEATURES], F32)
+            norms = prep.tile([P, 2 * TILES], F32)
+            nc.scalar.activation(out=squares[:], in_=rows, func=ACT.Square)
+            nc.vector.tensor_reduce(out=norms[:], in_=squares[:], axis=AXIS.X, op=ALU.add)
+            half_norms = prep.tile([P, 2 * TILES], F32)
+            nc.vector.tensor_scalar(
+                out=half_norms[:], in0=norms[:], scalar1=0.5, scalar2=None, op0=ALU.mult
+            )
+            q_norms = half_norms[:, 0:TILES]
+            k_norms = half_norms[:, TILES : 2 * TILES]
+
+            largest_of_8 = prep.tile([P, 1], F32)
+            nc.vector.tensor_reduce(out=largest_of_8[:], in_=q_norms, axis=AXIS.X, op=ALU.max)
+            spread_largest = turn_banks.tile([P, P], F32, tag="turn")
+            nc.tensor.transpose(
+                spread_largest[:], largest_of_8[:, 0:1].to_broadcast([P, P]), ident_f32[:]
+            )
+            shift = prep.tile([P, 1], F32)
+            nc.vector.tensor_reduce(out=shift[:], in_=spread_largest[:], axis=AXIS.X, op=ALU.max)
+
+            q_factor = prep.tile([P, TILES], F32)
+            nc.scalar.activation(
+                out=q_factor[:], in_=q_norms, func=ACT.Exp, bias=shift[:, 0:1], scale=-1.0
+            )
+            key_bias = prep.tile([P, TILES], F32)
+            nc.vector.scalar_tensor_tensor(
+                out=key_bias[:],
+                in0=mask_term[:, b * TILES : (b + 1) * TILES],
+                scalar=shift[:, 0:1],
+                in1=k_norms,
+                op0=ALU.subtract,
+                op1=ALU.subtract,
+            )
+
+            out_rows = prep.tile([P, TILES, FEATURES], F32)
+            return {
+                "qT": turned[0],
+                "kT": turned[1],
+                "q_factor": q_factor,
+                "key_bias": key_bias,
+                "v_codes": v_codes,
+                "v_scales": v_scales,
+                "out_rows": out_rows,
+            }
+
+        def attend(ready, half):
+            first = half * Q_TILES_PER_HALF
+            queries = ready["qT"][:, first : first + Q_TILES_PER_HALF, :].rearrange(
+                "d j p -> d (j p)"
+            )
+            spread_factor = factor_banks.tile([P, Q_HALF], F32)
+            for i in range(Q_TILES_PER_HALF):
+                nc.tensor.transpose(
+                    spread_factor[:, i * P : (i + 1) * P],
+                    ready["q_factor"][:, first + i : first + i + 1].to_broadcast([P, P]),
+                    ident_f32[:],
+                )
+
+            attn_codes = work.tile([P, PASSES, Q_HALF], U32, align_bytes=64)
+            attn_scales = work.tile([P, PASSES, Q_HALF], U8, align_bytes=64)
+            for c in range(PASSES):
+                key_part = work.tile([P, PACK, Q_HALF], F32)
+                for t in range(PACK):
+                    tile_index = c * PACK + t
+                    score = score_banks.tile([P, Q_HALF], F32)
+                    nc.tensor.matmul(
+                        score[:],
+                        lhsT=ready["kT"][:, tile_index, :],
+                        rhs=queries,
+                        start=True,
+                        stop=True,
+                    )
+                    nc.scalar.activation(
+                        out=key_part[:, t, :],
+                        in_=score[:],
+                        func=ACT.Exp,
+                        bias=ready["key_bias"][:, tile_index : tile_index + 1],
+                    )
+                attn = work.tile([P, Q_HALF, PACK], BF16, align_bytes=64)
+                nc.vector.tensor_tensor(
+                    out=attn[:].rearrange("p (g i) t -> p g t i", i=RUN),
+                    in0=key_part[:].rearrange("p t (g i) -> p g t i", i=RUN),
+                    in1=spread_factor[:]
+                    .rearrange("p (g i) -> p g i", i=RUN)
+                    .unsqueeze(2)
+                    .to_broadcast([P, Q_HALF // RUN, PACK, RUN]),
+                    op=ALU.mult,
+                )
+                nc.vector.quantize_mx(
+                    out=attn_codes[:, c, :].bitcast(FP8X4),
+                    scales=attn_scales[:, c, :],
+                    in_=attn[:].rearrange("p n t -> p (n t)"),
+                )
+
+            out_sums = out_banks.tile([P, Q_TILES_PER_HALF, FEATURES], F32)
+            for i in range(Q_TILES_PER_HALF):
+                for c in range(PASSES):
+                    nc.tensor.matmul_mx(
+                        out=out_sums[:, i, :],
+                        lhsT=attn_codes[:, c, i * P : (i + 1) * P].bitcast(FP8X4),
+                        lhsT_scale=attn_scales[:, c, i * P : (i + 1) * P],
+                        rhs=ready["v_codes"][:, c, :].bitcast(FP8X4),
+                        rhs_scale=ready["v_scales"][:, c, :],
+                        start=(c == 0),
+                        stop=(c == PASSES - 1),
+                    )
+            nc.scalar.copy(
+                out=ready["out_rows"][:, first : first + Q_TILES_PER_HALF, :], in_=out_sums[:]
+            )
+
+        def store(head, ready):
+            b, h = divmod(head, HEADS)
+            nc.sync.dma_start(
+                out=out[b, h].rearrange("(p j) f -> p j f", j=TILES), in_=ready["out_rows"][:]
+            )
+
+        n_heads = BATCHES * HEADS
+        loaded = {0: load(0), 1: load(1)}
+        ready = {0: prepare(0, loaded[0])}
+        for head in range(n_heads):
+            attend(ready[head], 0)
+            if head + 2 < n_heads:
+                loaded[head + 2] = load(head + 2)
+            if head + 1 < n_heads:
+                ready[head + 1] = prepare(head + 1, loaded[head + 1])
+            attend(ready[head], 1)
+            store(head, ready[head])

@@ -22,6 +22,8 @@ Q_HALF = 512
 HALVES = TOKENS // Q_HALF
 Q_TILES_PER_HALF = Q_HALF // P
 RUN = 4
+Q_VECTOR = 384
+Q_GPSIMD = Q_HALF - Q_VECTOR
 MASK_BIAS = 1.0e9
 
 FLOPS = 2 * 2 * BATCHES * HEADS * TOKENS * TOKENS * FEATURES
@@ -34,6 +36,7 @@ def tile_softmaxattention_kde_pa_t_kernel(tc, q_s, k_s, v_s, mask, out):
         inputs = ctx.enter_context(tc.tile_pool(name="inputs", bufs=3))
         prep = ctx.enter_context(tc.tile_pool(name="prep", bufs=2))
         work = ctx.enter_context(tc.tile_pool(name="work", bufs=3))
+        single = ctx.enter_context(tc.tile_pool(name="single", bufs=1))
         score_banks = ctx.enter_context(tc.psum_pool(name="score_banks", bufs=3))
         factor_banks = ctx.enter_context(tc.psum_pool(name="factor_banks", bufs=2))
         out_banks = ctx.enter_context(tc.psum_pool(name="out_banks", bufs=1))
@@ -164,8 +167,12 @@ def tile_softmaxattention_kde_pa_t_kernel(tc, q_s, k_s, v_s, mask, out):
                     ident_f32[:],
                 )
 
+            factor_sb = work.tile([P, Q_GPSIMD], F32)
+            nc.vector.tensor_copy(out=factor_sb[:], in_=spread_factor[:, Q_VECTOR:Q_HALF])
+
             attn_codes = work.tile([P, PASSES, Q_HALF], U32, align_bytes=64)
             attn_scales = work.tile([P, PASSES, Q_HALF], U8, align_bytes=64)
+            attn = single.tile([P, PASSES, Q_HALF, PACK], BF16, align_bytes=64)
             for c in range(PASSES):
                 key_part = work.tile([P, PACK, Q_HALF], F32)
                 for t in range(PACK):
@@ -184,21 +191,29 @@ def tile_softmaxattention_kde_pa_t_kernel(tc, q_s, k_s, v_s, mask, out):
                         func=ACT.Exp,
                         bias=ready["key_bias"][:, tile_index : tile_index + 1],
                     )
-                attn = work.tile([P, Q_HALF, PACK], BF16, align_bytes=64)
-                nc.vector.tensor_tensor(
-                    out=attn[:].rearrange("p (g i) t -> p g t i", i=RUN),
-                    in0=key_part[:].rearrange("p t (g i) -> p g t i", i=RUN),
-                    in1=spread_factor[:]
+                nc.gpsimd.tensor_tensor(
+                    out=attn[:, c, Q_VECTOR:Q_HALF, :].rearrange("p (g i) t -> p g t i", i=RUN),
+                    in0=key_part[:, :, Q_VECTOR:Q_HALF].rearrange("p t (g i) -> p g t i", i=RUN),
+                    in1=factor_sb[:]
                     .rearrange("p (g i) -> p g i", i=RUN)
                     .unsqueeze(2)
-                    .to_broadcast([P, Q_HALF // RUN, PACK, RUN]),
+                    .to_broadcast([P, Q_GPSIMD // RUN, PACK, RUN]),
                     op=ALU.mult,
                 )
-                nc.vector.quantize_mx(
-                    out=attn_codes[:, c, :].bitcast(FP8X4),
-                    scales=attn_scales[:, c, :],
-                    in_=attn[:].rearrange("p n t -> p (n t)"),
+                nc.vector.tensor_tensor(
+                    out=attn[:, c, 0:Q_VECTOR, :].rearrange("p (g i) t -> p g t i", i=RUN),
+                    in0=key_part[:, :, 0:Q_VECTOR].rearrange("p t (g i) -> p g t i", i=RUN),
+                    in1=spread_factor[:, 0:Q_VECTOR]
+                    .rearrange("p (g i) -> p g i", i=RUN)
+                    .unsqueeze(2)
+                    .to_broadcast([P, Q_VECTOR // RUN, PACK, RUN]),
+                    op=ALU.mult,
                 )
+            nc.vector.quantize_mx(
+                out=attn_codes[:].rearrange("p c n -> p (c n)").bitcast(FP8X4),
+                scales=attn_scales[:].rearrange("p c n -> p (c n)"),
+                in_=attn[:].rearrange("p c n t -> p (c n t)"),
+            )
 
             out_sums = out_banks.tile([P, Q_TILES_PER_HALF, FEATURES], F32)
             for i in range(Q_TILES_PER_HALF):

@@ -94,7 +94,7 @@ def tile_softmaxattention_kde_pa_t_kernel(tc, q_s, k_s, v_s, mask, out):
                 for j in range(TILES):
                     nc.tensor.transpose(turned_bank[:, j, :], qk[:, a, j, :], ident_bf16[:])
                 turned_sb = prep.tile([P, TILES, P], BF16, name="turned%d" % a)
-                nc.scalar.copy(out=turned_sb[:], in_=turned_bank[:])
+                nc.vector.tensor_copy(out=turned_sb[:], in_=turned_bank[:])
                 turned.append(turned_sb)
 
             v_grouped = prep.tile([P, PASSES, FEATURES, PACK], BF16, align_bytes=64)
@@ -109,10 +109,15 @@ def tile_softmaxattention_kde_pa_t_kernel(tc, q_s, k_s, v_s, mask, out):
                 in_=v_grouped[:].rearrange("p c w t -> p (c w t)"),
             )
             rows = qk[:].rearrange("p a j d -> p (a j) d")
-            squares = prep.tile([P, 2 * TILES, FEATURES], F32)
             norms = prep.tile([P, 2 * TILES], F32)
-            nc.scalar.activation(out=squares[:], in_=rows, func=ACT.Square)
-            nc.vector.tensor_reduce(out=norms[:], in_=squares[:], axis=AXIS.X, op=ALU.add)
+            for column in range(2 * TILES):
+                squares = prep.tile([P, FEATURES], BF16)
+                nc.scalar.activation(
+                    out=squares[:],
+                    in_=rows[:, column, :],
+                    func=ACT.Square,
+                    accum_out=norms[:, column : column + 1],
+                )
             half_norms = prep.tile([P, 2 * TILES], F32)
             nc.vector.tensor_scalar(
                 out=half_norms[:], in0=norms[:], scalar1=0.5, scalar2=None, op0=ALU.mult
@@ -227,9 +232,14 @@ def tile_softmaxattention_kde_pa_t_kernel(tc, q_s, k_s, v_s, mask, out):
                         start=(c == 0),
                         stop=(c == PASSES - 1),
                     )
-            nc.scalar.copy(
-                out=ready["out_rows"][:, first : first + Q_TILES_PER_HALF, :], in_=out_sums[:]
-            )
+            if half == 0:
+                nc.vector.tensor_copy(
+                    out=ready["out_rows"][:, first : first + Q_TILES_PER_HALF, :], in_=out_sums[:]
+                )
+            else:
+                nc.scalar.copy(
+                    out=ready["out_rows"][:, first : first + Q_TILES_PER_HALF, :], in_=out_sums[:]
+                )
 
         def store(head, ready):
             b, h = divmod(head, HEADS)

@@ -31,10 +31,12 @@ FLOPS = 2 * 2 * BATCHES * HEADS * TOKENS * TOKENS * FEATURES
 
 def tile_softmaxattention_kde_pa_t_kernel(tc, q_s, k_s, v_s, mask, out):
     nc = tc.nc
+    n_heads = BATCHES * HEADS
+    n_steps = n_heads * HALVES
     with ExitStack() as ctx:
         const = ctx.enter_context(tc.tile_pool(name="const", bufs=1))
-        inputs = ctx.enter_context(tc.tile_pool(name="inputs", bufs=3))
-        prep = ctx.enter_context(tc.tile_pool(name="prep", bufs=2))
+        inputs = ctx.enter_context(tc.tile_pool(name="inputs", bufs=4))
+        prep = ctx.enter_context(tc.tile_pool(name="prep", bufs=3))
         work = ctx.enter_context(tc.tile_pool(name="work", bufs=3))
         single = ctx.enter_context(tc.tile_pool(name="single", bufs=1))
         score_banks = ctx.enter_context(tc.psum_pool(name="score_banks", bufs=3))
@@ -51,21 +53,8 @@ def tile_softmaxattention_kde_pa_t_kernel(tc, q_s, k_s, v_s, mask, out):
         nc.vector.memset(warm[:], 0.0)
         nc.scalar.activation(out=warm[:], in_=warm[:], func=ACT.Exp)
 
-        mask_rows = const.tile([P, BATCHES * PASSES, PACK], BF16)
-        with nc.allow_non_contiguous_dma(reason="the mask is 8 KiB, loaded once, 4 keys a run"):
-            nc.sync.dma_start(
-                out=mask_rows[:],
-                in_=mask.rearrange("b (c p t) -> p (b c) t", c=PASSES, t=PACK),
-            )
-        mask_term = const.tile([P, BATCHES * TILES], F32)
-        nc.vector.tensor_scalar(
-            out=mask_term[:],
-            in0=mask_rows[:].rearrange("p a t -> p (a t)"),
-            scalar1=MASK_BIAS,
-            scalar2=-MASK_BIAS,
-            op0=ALU.mult,
-            op1=ALU.add,
-        )
+        heads = {}
+        steps = {}
 
         def load(head):
             b, h = divmod(head, HEADS)
@@ -82,179 +71,355 @@ def tile_softmaxattention_kde_pa_t_kernel(tc, q_s, k_s, v_s, mask, out):
                 out=v_rows[:],
                 in_=v_s[b, h].rearrange("(c p t) d -> p c t d", c=PASSES, t=PACK),
             )
-            return {"qk": qk, "v_rows": v_rows}
+            heads[head] = {"qk": qk, "v_rows": v_rows}
 
-        def prepare(head, loaded):
-            b = head // HEADS
-            qk = loaded["qk"]
+        load(0)
+        load(1)
 
-            turned = []
-            for a in range(2):
-                turned_bank = turn_banks.tile([P, TILES, P], BF16, tag="turn")
-                for j in range(TILES):
-                    nc.tensor.transpose(turned_bank[:, j, :], qk[:, a, j, :], ident_bf16[:])
-                turned_sb = prep.tile([P, TILES, P], BF16, name="turned%d" % a)
-                nc.vector.tensor_copy(out=turned_sb[:], in_=turned_bank[:])
-                turned.append(turned_sb)
-
-            v_grouped = prep.tile([P, PASSES, FEATURES, PACK], BF16, align_bytes=64)
-            nc.vector.tensor_copy(
-                out=v_grouped[:], in_=loaded["v_rows"][:].rearrange("p c t w -> p c w t")
+        mask_rows = const.tile([P, BATCHES * PASSES, PACK], BF16)
+        with nc.allow_non_contiguous_dma(reason="the mask is 8 KiB, loaded once, 4 keys a run"):
+            nc.scalar.dma_start(
+                out=mask_rows[:],
+                in_=mask.rearrange("b (c p t) -> p (b c) t", c=PASSES, t=PACK),
             )
-            v_codes = prep.tile([P, PASSES, FEATURES], U32, align_bytes=64)
-            v_scales = prep.tile([P, PASSES, FEATURES], U8, align_bytes=64)
-            nc.vector.quantize_mx(
-                out=v_codes[:].rearrange("p c w -> p (c w)").bitcast(FP8X4),
-                scales=v_scales[:].rearrange("p c w -> p (c w)"),
-                in_=v_grouped[:].rearrange("p c w t -> p (c w t)"),
-            )
-            rows = qk[:].rearrange("p a j d -> p (a j) d")
-            norms = prep.tile([P, 2 * TILES], F32)
-            for column in range(2 * TILES):
+        mask_term = const.tile([P, BATCHES * TILES], F32)
+        nc.vector.tensor_scalar(
+            out=mask_term[:],
+            in0=mask_rows[:].rearrange("p a t -> p (a t)"),
+            scalar1=MASK_BIAS,
+            scalar2=-MASK_BIAS,
+            op0=ALU.mult,
+            op1=ALU.add,
+        )
+        load(2)
+
+
+        def square_sums(head, columns):
+            tiles = heads[head]
+            if "norms" not in tiles:
+                norms = prep.tile([P, 2 * TILES], F32)
+                tiles["norms"] = norms
+            rows = tiles["qk"][:].rearrange("p a j d -> p (a j) d")
+            for column in columns:
                 squares = prep.tile([P, FEATURES], BF16)
                 nc.scalar.activation(
                     out=squares[:],
                     in_=rows[:, column, :],
                     func=ACT.Square,
-                    accum_out=norms[:, column : column + 1],
+                    accum_out=tiles["norms"][:, column : column + 1],
                 )
+
+        def square_sums_by_vector(head, first_column, n_columns):
+            tiles = heads[head]
+            if "norms" not in tiles:
+                norms = prep.tile([P, 2 * TILES], F32)
+                tiles["norms"] = norms
+            rows = tiles["qk"][:].rearrange("p a j d -> p (a j) d")
+            stats = prep.tile([P, n_columns, 2, 3], F32)
+            for i in range(n_columns):
+                nc.vector.bn_stats(
+                    out=stats[:, i].rearrange("p e s -> p (e s)"), in_=rows[:, first_column + i, :]
+                )
+            mean_squares = prep.tile([P, n_columns, 2], F32)
+            nc.vector.tensor_tensor(
+                out=mean_squares[:], in0=stats[:, :, :, 1], in1=stats[:, :, :, 1], op=ALU.mult
+            )
+            half_sums = prep.tile([P, n_columns, 2], F32)
+            nc.vector.scalar_tensor_tensor(
+                out=half_sums[:],
+                in0=mean_squares[:],
+                scalar=float(FEATURES // 2),
+                in1=stats[:, :, :, 2],
+                op0=ALU.mult,
+                op1=ALU.add,
+            )
+            nc.vector.tensor_reduce(
+                out=tiles["norms"][:, first_column : first_column + n_columns],
+                in_=half_sums[:],
+                axis=AXIS.X,
+                op=ALU.add,
+            )
+
+        def halve(head):
+            tiles = heads[head]
             half_norms = prep.tile([P, 2 * TILES], F32)
-            nc.vector.tensor_scalar(
-                out=half_norms[:], in0=norms[:], scalar1=0.5, scalar2=None, op0=ALU.mult
+            nc.gpsimd.tensor_scalar(
+                out=half_norms[:],
+                in0=tiles["norms"][:],
+                scalar1=0.5,
+                scalar2=0.0,
+                op0=ALU.mult,
+                op1=ALU.add,
             )
-            q_norms = half_norms[:, 0:TILES]
-            k_norms = half_norms[:, TILES : 2 * TILES]
+            tiles["half_norms"] = half_norms
 
+        def largest_in_partition(head):
+            tiles = heads[head]
             largest_of_8 = prep.tile([P, 1], F32)
-            nc.vector.tensor_reduce(out=largest_of_8[:], in_=q_norms, axis=AXIS.X, op=ALU.max)
-            spread_largest = turn_banks.tile([P, P], F32, tag="turn")
-            nc.tensor.transpose(
-                spread_largest[:], largest_of_8[:, 0:1].to_broadcast([P, P]), ident_f32[:]
+            nc.vector.tensor_reduce(
+                out=largest_of_8[:], in_=tiles["half_norms"][:, 0:TILES], axis=AXIS.X, op=ALU.max
             )
-            shift = prep.tile([P, 1], F32)
-            nc.vector.tensor_reduce(out=shift[:], in_=spread_largest[:], axis=AXIS.X, op=ALU.max)
+            tiles["largest_of_8"] = largest_of_8
 
+        def spread_largest(head):
+            tiles = heads[head]
+            spread = turn_banks.tile([P, P], F32, tag="turn")
+            nc.tensor.transpose(
+                spread[:], tiles["largest_of_8"][:, 0:1].to_broadcast([P, P]), ident_f32[:]
+            )
+            tiles["spread_largest"] = spread
+
+        def largest_of_head(head):
+            tiles = heads[head]
+            shift = prep.tile([P, 1], F32)
+            nc.vector.tensor_reduce(
+                out=shift[:], in_=tiles["spread_largest"][:], axis=AXIS.X, op=ALU.max
+            )
+            tiles["shift"] = shift
+
+        def query_factor(head):
+            tiles = heads[head]
             q_factor = prep.tile([P, TILES], F32)
             nc.scalar.activation(
-                out=q_factor[:], in_=q_norms, func=ACT.Exp, bias=shift[:, 0:1], scale=-1.0
+                out=q_factor[:],
+                in_=tiles["half_norms"][:, 0:TILES],
+                func=ACT.Exp,
+                bias=tiles["shift"][:, 0:1],
+                scale=-1.0,
             )
-            key_bias = prep.tile([P, TILES], F32)
-            nc.vector.scalar_tensor_tensor(
-                out=key_bias[:],
+            tiles["q_factor"] = q_factor
+
+        def key_bias(head):
+            tiles = heads[head]
+            b = head // HEADS
+            shifted = prep.tile([P, TILES], F32)
+            nc.gpsimd.tensor_scalar(
+                out=shifted[:],
                 in0=mask_term[:, b * TILES : (b + 1) * TILES],
-                scalar=shift[:, 0:1],
-                in1=k_norms,
+                scalar1=tiles["shift"][:, 0:1],
+                scalar2=0.0,
                 op0=ALU.subtract,
-                op1=ALU.subtract,
+                op1=ALU.add,
             )
+            bias = prep.tile([P, TILES], F32)
+            nc.gpsimd.tensor_tensor(
+                out=bias[:],
+                in0=shifted[:],
+                in1=tiles["half_norms"][:, TILES : 2 * TILES],
+                op=ALU.subtract,
+            )
+            tiles["key_bias"] = bias
 
-            out_rows = prep.tile([P, TILES, FEATURES], F32)
-            return {
-                "qT": turned[0],
-                "kT": turned[1],
-                "q_factor": q_factor,
-                "key_bias": key_bias,
-                "v_codes": v_codes,
-                "v_scales": v_scales,
-                "out_rows": out_rows,
-            }
+        def turn(head, a):
+            tiles = heads[head]
+            turned_bank = turn_banks.tile([P, TILES, P], BF16, tag="turn")
+            for j in range(TILES):
+                nc.tensor.transpose(turned_bank[:, j, :], tiles["qk"][:, a, j, :], ident_bf16[:])
+            tiles["turned_bank%d" % a] = turned_bank
 
-        def attend(ready, half):
+        def turn_copy(head, a):
+            tiles = heads[head]
+            turned_sb = prep.tile([P, TILES, P], BF16, name="turned%d" % a)
+            nc.vector.tensor_copy(out=turned_sb[:], in_=tiles["turned_bank%d" % a][:])
+            tiles["turned%d" % a] = turned_sb
+
+        def v_group(head):
+            tiles = heads[head]
+            v_grouped = prep.tile([P, PASSES, FEATURES, PACK], BF16, align_bytes=64)
+            nc.vector.tensor_copy(
+                out=v_grouped[:], in_=tiles["v_rows"][:].rearrange("p c t w -> p c w t")
+            )
+            tiles["v_grouped"] = v_grouped
+
+        def v_quantize(head):
+            tiles = heads[head]
+            v_codes = prep.tile([P, PASSES, FEATURES], U32, align_bytes=64)
+            v_scales = prep.tile([P, PASSES, FEATURES], U8, align_bytes=64)
+            nc.vector.quantize_mx(
+                out=v_codes[:].rearrange("p c w -> p (c w)").bitcast(FP8X4),
+                scales=v_scales[:].rearrange("p c w -> p (c w)"),
+                in_=tiles["v_grouped"][:].rearrange("p c w t -> p (c w t)"),
+            )
+            tiles["v_codes"] = v_codes
+            tiles["v_scales"] = v_scales
+
+
+        def scores_and_exp(step, tile_index):
+            head, half = divmod(step, HALVES)
+            tiles = heads[head]
             first = half * Q_TILES_PER_HALF
-            queries = ready["qT"][:, first : first + Q_TILES_PER_HALF, :].rearrange(
-                "d j p -> d (j p)"
+            c, t = divmod(tile_index, PACK)
+            if t == 0:
+                key_part = work.tile([P, PACK, Q_HALF], F32)
+                steps[step]["key_part%d" % c] = key_part
+            score = score_banks.tile([P, Q_HALF], F32)
+            nc.tensor.matmul(
+                score[:],
+                lhsT=tiles["turned1"][:, tile_index, :],
+                rhs=tiles["turned0"][:, first : first + Q_TILES_PER_HALF, :].rearrange(
+                    "d j p -> d (j p)"
+                ),
+                start=True,
+                stop=True,
             )
-            spread_factor = factor_banks.tile([P, Q_HALF], F32)
+            nc.scalar.activation(
+                out=steps[step]["key_part%d" % c][:, t, :],
+                in_=score[:],
+                func=ACT.Exp,
+                bias=tiles["key_bias"][:, tile_index : tile_index + 1],
+            )
+
+        def spread_factor(step):
+            head, half = divmod(step, HALVES)
+            first = half * Q_TILES_PER_HALF
+            spread = factor_banks.tile([P, Q_HALF], F32)
             for i in range(Q_TILES_PER_HALF):
                 nc.tensor.transpose(
-                    spread_factor[:, i * P : (i + 1) * P],
-                    ready["q_factor"][:, first + i : first + i + 1].to_broadcast([P, P]),
+                    spread[:, i * P : (i + 1) * P],
+                    heads[head]["q_factor"][:, first + i : first + i + 1].to_broadcast([P, P]),
                     ident_f32[:],
                 )
+            steps[step]["spread"] = spread
 
+        def factor_copy(step):
             factor_sb = work.tile([P, Q_GPSIMD], F32)
-            nc.vector.tensor_copy(out=factor_sb[:], in_=spread_factor[:, Q_VECTOR:Q_HALF])
+            nc.vector.tensor_copy(out=factor_sb[:], in_=steps[step]["spread"][:, Q_VECTOR:Q_HALF])
+            steps[step]["factor_sb"] = factor_sb
 
+        def multiply(step, c):
+            tiles = steps[step]
+            if c == 0:
+                attn = single.tile([P, PASSES, Q_HALF, PACK], BF16, align_bytes=64)
+                tiles["attn"] = attn
+            attn = tiles["attn"]
+            key_part = tiles["key_part%d" % c]
+            nc.gpsimd.tensor_tensor(
+                out=attn[:, c, Q_VECTOR:Q_HALF, :].rearrange("p (g i) t -> p g t i", i=RUN),
+                in0=key_part[:, :, Q_VECTOR:Q_HALF].rearrange("p t (g i) -> p g t i", i=RUN),
+                in1=tiles["factor_sb"][:]
+                .rearrange("p (g i) -> p g i", i=RUN)
+                .unsqueeze(2)
+                .to_broadcast([P, Q_GPSIMD // RUN, PACK, RUN]),
+                op=ALU.mult,
+            )
+            nc.vector.tensor_tensor(
+                out=attn[:, c, 0:Q_VECTOR, :].rearrange("p (g i) t -> p g t i", i=RUN),
+                in0=key_part[:, :, 0:Q_VECTOR].rearrange("p t (g i) -> p g t i", i=RUN),
+                in1=tiles["spread"][:, 0:Q_VECTOR]
+                .rearrange("p (g i) -> p g i", i=RUN)
+                .unsqueeze(2)
+                .to_broadcast([P, Q_VECTOR // RUN, PACK, RUN]),
+                op=ALU.mult,
+            )
+
+        def quantize(step):
+            tiles = steps[step]
             attn_codes = work.tile([P, PASSES, Q_HALF], U32, align_bytes=64)
             attn_scales = work.tile([P, PASSES, Q_HALF], U8, align_bytes=64)
-            attn = single.tile([P, PASSES, Q_HALF, PACK], BF16, align_bytes=64)
-            for c in range(PASSES):
-                key_part = work.tile([P, PACK, Q_HALF], F32)
-                for t in range(PACK):
-                    tile_index = c * PACK + t
-                    score = score_banks.tile([P, Q_HALF], F32)
-                    nc.tensor.matmul(
-                        score[:],
-                        lhsT=ready["kT"][:, tile_index, :],
-                        rhs=queries,
-                        start=True,
-                        stop=True,
-                    )
-                    nc.scalar.activation(
-                        out=key_part[:, t, :],
-                        in_=score[:],
-                        func=ACT.Exp,
-                        bias=ready["key_bias"][:, tile_index : tile_index + 1],
-                    )
-                nc.gpsimd.tensor_tensor(
-                    out=attn[:, c, Q_VECTOR:Q_HALF, :].rearrange("p (g i) t -> p g t i", i=RUN),
-                    in0=key_part[:, :, Q_VECTOR:Q_HALF].rearrange("p t (g i) -> p g t i", i=RUN),
-                    in1=factor_sb[:]
-                    .rearrange("p (g i) -> p g i", i=RUN)
-                    .unsqueeze(2)
-                    .to_broadcast([P, Q_GPSIMD // RUN, PACK, RUN]),
-                    op=ALU.mult,
-                )
-                nc.vector.tensor_tensor(
-                    out=attn[:, c, 0:Q_VECTOR, :].rearrange("p (g i) t -> p g t i", i=RUN),
-                    in0=key_part[:, :, 0:Q_VECTOR].rearrange("p t (g i) -> p g t i", i=RUN),
-                    in1=spread_factor[:, 0:Q_VECTOR]
-                    .rearrange("p (g i) -> p g i", i=RUN)
-                    .unsqueeze(2)
-                    .to_broadcast([P, Q_VECTOR // RUN, PACK, RUN]),
-                    op=ALU.mult,
-                )
             nc.vector.quantize_mx(
                 out=attn_codes[:].rearrange("p c n -> p (c n)").bitcast(FP8X4),
                 scales=attn_scales[:].rearrange("p c n -> p (c n)"),
-                in_=attn[:].rearrange("p c n t -> p (c n t)"),
+                in_=tiles["attn"][:].rearrange("p c n t -> p (c n t)"),
             )
+            tiles["attn_codes"] = attn_codes
+            tiles["attn_scales"] = attn_scales
 
+        def attn_times_v(step):
+            head = step // HALVES
+            tiles = steps[step]
             out_sums = out_banks.tile([P, Q_TILES_PER_HALF, FEATURES], F32)
             for i in range(Q_TILES_PER_HALF):
                 for c in range(PASSES):
                     nc.tensor.matmul_mx(
                         out=out_sums[:, i, :],
-                        lhsT=attn_codes[:, c, i * P : (i + 1) * P].bitcast(FP8X4),
-                        lhsT_scale=attn_scales[:, c, i * P : (i + 1) * P],
-                        rhs=ready["v_codes"][:, c, :].bitcast(FP8X4),
-                        rhs_scale=ready["v_scales"][:, c, :],
+                        lhsT=tiles["attn_codes"][:, c, i * P : (i + 1) * P].bitcast(FP8X4),
+                        lhsT_scale=tiles["attn_scales"][:, c, i * P : (i + 1) * P],
+                        rhs=heads[head]["v_codes"][:, c, :].bitcast(FP8X4),
+                        rhs_scale=heads[head]["v_scales"][:, c, :],
                         start=(c == 0),
                         stop=(c == PASSES - 1),
                     )
+            tiles["out_sums"] = out_sums
+
+        def out_copy(step):
+            head, half = divmod(step, HALVES)
+            first = half * Q_TILES_PER_HALF
             if half == 0:
-                nc.vector.tensor_copy(
-                    out=ready["out_rows"][:, first : first + Q_TILES_PER_HALF, :], in_=out_sums[:]
-                )
-            else:
-                nc.scalar.copy(
-                    out=ready["out_rows"][:, first : first + Q_TILES_PER_HALF, :], in_=out_sums[:]
-                )
-
-        def store(head, ready):
-            b, h = divmod(head, HEADS)
-            nc.sync.dma_start(
-                out=out[b, h].rearrange("(p j) f -> p j f", j=TILES), in_=ready["out_rows"][:]
+                out_rows = prep.tile([P, TILES, FEATURES], F32)
+                heads[head]["out_rows"] = out_rows
+            nc.vector.tensor_copy(
+                out=heads[head]["out_rows"][:, first : first + Q_TILES_PER_HALF, :],
+                in_=steps[step]["out_sums"][:],
             )
+            if half == HALVES - 1:
+                b, h = divmod(head, HEADS)
+                nc.sync.dma_start(
+                    out=out[b, h].rearrange("(p j) f -> p j f", j=TILES),
+                    in_=heads[head]["out_rows"][:],
+                )
 
-        n_heads = BATCHES * HEADS
-        loaded = {0: load(0), 1: load(1)}
-        ready = {0: prepare(0, loaded[0])}
-        for head in range(n_heads):
-            attend(ready[head], 0)
-            if head + 2 < n_heads:
-                loaded[head + 2] = load(head + 2)
-            if head + 1 < n_heads:
-                ready[head + 1] = prepare(head + 1, loaded[head + 1])
-            attend(ready[head], 1)
-            store(head, ready[head])
+        ctx.enter_context(tc.manual_schedule())
+
+        turn(0, 0)
+        turn(0, 1)
+        square_sums(0, range(TILES))
+        square_sums_by_vector(0, TILES, TILES)
+        halve(0)
+        largest_in_partition(0)
+        turn_copy(0, 0)
+        spread_largest(0)
+        largest_of_head(0)
+        turn_copy(0, 1)
+        key_bias(0)
+        query_factor(0)
+        v_group(0)
+        square_sums_by_vector(1, 0, 2 * TILES)
+        v_quantize(0)
+
+        for step in range(n_steps):
+            second = step % HALVES == 1
+            steps[step] = {}
+            squares_head = (step + 3) // HALVES if second else step // HALVES + 2
+            turn_head = n_heads if second else step // HALVES + 1
+            last_head = (step + 1) // HALVES if second else n_heads
+            load_head = n_heads if second else step // HALVES + 3
+
+            if load_head < n_heads:
+                load(load_head)
+            if turn_head < n_heads:
+                halve(turn_head)
+                largest_in_partition(turn_head)
+            if last_head < n_heads:
+                key_bias(last_head)
+            for tile_index in range(TILES):
+                scores_and_exp(step, tile_index)
+                if squares_head < n_heads:
+                    square_sums(squares_head, [tile_index + (TILES if second else 0)])
+                if tile_index == 1 and turn_head < n_heads:
+                    turn(turn_head, 0)
+                    turn_copy(turn_head, 0)
+                if tile_index == 2:
+                    spread_factor(step)
+                if tile_index == 3:
+                    if turn_head < n_heads:
+                        turn(turn_head, 1)
+                    factor_copy(step)
+                    multiply(step, 0)
+                    if turn_head < n_heads:
+                        turn_copy(turn_head, 1)
+                if tile_index == 6 and last_head < n_heads:
+                    query_factor(last_head)
+            multiply(step, 1)
+            if step > 0:
+                attn_times_v(step - 1)
+                out_copy(step - 1)
+            if turn_head < n_heads:
+                spread_largest(turn_head)
+                largest_of_head(turn_head)
+            if last_head < n_heads:
+                v_group(last_head)
+            quantize(step)
+            if last_head < n_heads:
+                v_quantize(last_head)
+        attn_times_v(n_steps - 1)
+        out_copy(n_steps - 1)

@@ -22,7 +22,7 @@ Q_HALF = 512
 HALVES = TOKENS // Q_HALF
 Q_TILES_PER_HALF = Q_HALF // P
 RUN = 4
-Q_VECTOR = 384
+Q_VECTOR = 352
 Q_GPSIMD = Q_HALF - Q_VECTOR
 MASK_BIAS = 1.0e9
 
@@ -143,13 +143,8 @@ def tile_softmaxattention_kde_pa_t_kernel(tc, q_s, k_s, v_s, mask, out):
         def halve(head):
             tiles = heads[head]
             half_norms = prep.tile([P, 2 * TILES], F32)
-            nc.gpsimd.tensor_scalar(
-                out=half_norms[:],
-                in0=tiles["norms"][:],
-                scalar1=0.5,
-                scalar2=0.0,
-                op0=ALU.mult,
-                op1=ALU.add,
+            nc.vector.tensor_scalar(
+                out=half_norms[:], in0=tiles["norms"][:], scalar1=0.5, scalar2=None, op0=ALU.mult
             )
             tiles["half_norms"] = half_norms
 
@@ -192,21 +187,14 @@ def tile_softmaxattention_kde_pa_t_kernel(tc, q_s, k_s, v_s, mask, out):
         def key_bias(head):
             tiles = heads[head]
             b = head // HEADS
-            shifted = prep.tile([P, TILES], F32)
-            nc.gpsimd.tensor_scalar(
-                out=shifted[:],
-                in0=mask_term[:, b * TILES : (b + 1) * TILES],
-                scalar1=tiles["shift"][:, 0:1],
-                scalar2=0.0,
-                op0=ALU.subtract,
-                op1=ALU.add,
-            )
             bias = prep.tile([P, TILES], F32)
-            nc.gpsimd.tensor_tensor(
+            nc.vector.scalar_tensor_tensor(
                 out=bias[:],
-                in0=shifted[:],
+                in0=mask_term[:, b * TILES : (b + 1) * TILES],
+                scalar=tiles["shift"][:, 0:1],
                 in1=tiles["half_norms"][:, TILES : 2 * TILES],
-                op=ALU.subtract,
+                op0=ALU.subtract,
+                op1=ALU.subtract,
             )
             tiles["key_bias"] = bias
 
@@ -283,7 +271,7 @@ def tile_softmaxattention_kde_pa_t_kernel(tc, q_s, k_s, v_s, mask, out):
 
         def factor_copy(step):
             factor_sb = work.tile([P, Q_GPSIMD], F32)
-            nc.vector.tensor_copy(out=factor_sb[:], in_=steps[step]["spread"][:, Q_VECTOR:Q_HALF])
+            nc.scalar.copy(out=factor_sb[:], in_=steps[step]["spread"][:, Q_VECTOR:Q_HALF])
             steps[step]["factor_sb"] = factor_sb
 
         def multiply(step, c):
@@ -371,9 +359,10 @@ def tile_softmaxattention_kde_pa_t_kernel(tc, q_s, k_s, v_s, mask, out):
         largest_of_head(0)
         turn_copy(0, 1)
         key_bias(0)
+        square_sums(1, range(TILES))
         query_factor(0)
         v_group(0)
-        square_sums_by_vector(1, 0, 2 * TILES)
+        square_sums_by_vector(1, TILES, TILES)
         v_quantize(0)
 
         for step in range(n_steps):
@@ -388,26 +377,26 @@ def tile_softmaxattention_kde_pa_t_kernel(tc, q_s, k_s, v_s, mask, out):
                 load(load_head)
             if turn_head < n_heads:
                 halve(turn_head)
-                largest_in_partition(turn_head)
             if last_head < n_heads:
                 key_bias(last_head)
             for tile_index in range(TILES):
                 scores_and_exp(step, tile_index)
                 if squares_head < n_heads:
                     square_sums(squares_head, [tile_index + (TILES if second else 0)])
-                if tile_index == 1 and turn_head < n_heads:
+                if tile_index == 0:
+                    spread_factor(step)
+                    factor_copy(step)
+                if tile_index == 2 and turn_head < n_heads:
                     turn(turn_head, 0)
                     turn_copy(turn_head, 0)
-                if tile_index == 2:
-                    spread_factor(step)
+                    largest_in_partition(turn_head)
                 if tile_index == 3:
                     if turn_head < n_heads:
                         turn(turn_head, 1)
-                    factor_copy(step)
                     multiply(step, 0)
                     if turn_head < n_heads:
                         turn_copy(turn_head, 1)
-                if tile_index == 6 and last_head < n_heads:
+                if tile_index == 5 and last_head < n_heads:
                     query_factor(last_head)
             multiply(step, 1)
             if step > 0:

@@ -22,7 +22,7 @@ Q_HALF = 512
 HALVES = TOKENS // Q_HALF
 Q_TILES_PER_HALF = Q_HALF // P
 RUN = 4
-Q_VECTOR = 352
+Q_VECTOR = 320
 Q_GPSIMD = Q_HALF - Q_VECTOR
 MASK_BIAS = 1.0e9
 
@@ -271,7 +271,12 @@ def tile_softmaxattention_kde_pa_t_kernel(tc, q_s, k_s, v_s, mask, out):
 
         def factor_copy(step):
             factor_sb = work.tile([P, Q_GPSIMD], F32)
-            nc.scalar.copy(out=factor_sb[:], in_=steps[step]["spread"][:, Q_VECTOR:Q_HALF])
+            if step % HALVES == 0:
+                nc.scalar.copy(out=factor_sb[:], in_=steps[step]["spread"][:, Q_VECTOR:Q_HALF])
+            else:
+                nc.vector.tensor_copy(
+                    out=factor_sb[:], in_=steps[step]["spread"][:, Q_VECTOR:Q_HALF]
+                )
             steps[step]["factor_sb"] = factor_sb
 
         def multiply(step, c):
@@ -367,7 +372,9 @@ def tile_softmaxattention_kde_pa_t_kernel(tc, q_s, k_s, v_s, mask, out):
 
         for step in range(n_steps):
             second = step % HALVES == 1
-            steps[step] = {}
+            if not second:
+                steps[step] = {}
+                steps[step + 1] = {}
             squares_head = (step + 3) // HALVES if second else step // HALVES + 2
             turn_head = n_heads if second else step // HALVES + 1
             last_head = (step + 1) // HALVES if second else n_heads
@@ -383,9 +390,11 @@ def tile_softmaxattention_kde_pa_t_kernel(tc, q_s, k_s, v_s, mask, out):
                 scores_and_exp(step, tile_index)
                 if squares_head < n_heads:
                     square_sums(squares_head, [tile_index + (TILES if second else 0)])
-                if tile_index == 0:
+                if tile_index == 0 and not second:
                     spread_factor(step)
                     factor_copy(step)
+                if tile_index == 5 and not second:
+                    spread_factor(step + 1)
                 if tile_index == 2 and turn_head < n_heads:
                     turn(turn_head, 0)
                     turn_copy(turn_head, 0)
@@ -399,6 +408,8 @@ def tile_softmaxattention_kde_pa_t_kernel(tc, q_s, k_s, v_s, mask, out):
                 if tile_index == 5 and last_head < n_heads:
                     query_factor(last_head)
             multiply(step, 1)
+            if not second:
+                factor_copy(step + 1)
             if step > 0:
                 attn_times_v(step - 1)
                 out_copy(step - 1)

@@ -1,3 +1,4 @@
+import math
 from contextlib import ExitStack
 
 import concourse.mybir as mybir
@@ -49,6 +50,14 @@ def tile_softmaxattention_kde_pa_t_kernel(tc, q_s, k_s, v_s, mask, out):
         ident_f32 = const.tile([P, P], F32)
         make_identity(nc, ident_f32[:])
 
+        mask_rows = const.tile([P, BATCHES * PASSES, PACK], BF16)
+        with nc.allow_non_contiguous_dma(reason="the mask is 8 KiB, loaded once, 4 keys a run"):
+            nc.scalar.dma_start(
+                out=mask_rows[:],
+                in_=mask.rearrange("b (c p t) -> p (b c) t", c=PASSES, t=PACK),
+            )
+        mask_term = const.tile([P, BATCHES * TILES], F32)
+
         warm = const.tile([P, 1], F32)
         nc.vector.memset(warm[:], 0.0)
         nc.scalar.activation(out=warm[:], in_=warm[:], func=ACT.Exp)
@@ -75,30 +84,29 @@ def tile_softmaxattention_kde_pa_t_kernel(tc, q_s, k_s, v_s, mask, out):
 
         load(0)
         load(1)
-
-        mask_rows = const.tile([P, BATCHES * PASSES, PACK], BF16)
-        with nc.allow_non_contiguous_dma(reason="the mask is 8 KiB, loaded once, 4 keys a run"):
-            nc.scalar.dma_start(
-                out=mask_rows[:],
-                in_=mask.rearrange("b (c p t) -> p (b c) t", c=PASSES, t=PACK),
-            )
-        mask_term = const.tile([P, BATCHES * TILES], F32)
-        nc.vector.tensor_scalar(
-            out=mask_term[:],
-            in0=mask_rows[:].rearrange("p a t -> p (a t)"),
-            scalar1=MASK_BIAS,
-            scalar2=-MASK_BIAS,
-            op0=ALU.mult,
-            op1=ALU.add,
-        )
         load(2)
 
+        def mask_terms():
+            nc.vector.tensor_scalar(
+                out=mask_term[:],
+                in0=mask_rows[:].rearrange("p a t -> p (a t)"),
+                scalar1=MASK_BIAS,
+                scalar2=-MASK_BIAS,
+                op0=ALU.mult,
+                op1=ALU.add,
+            )
+
+
+        def half_norms_tile(head):
+            tiles = heads[head]
+            if "half_norms" not in tiles:
+                half_norms = prep.tile([P, 2 * TILES], F32)
+                tiles["half_norms"] = half_norms
+            return tiles["half_norms"]
 
         def square_sums(head, columns):
             tiles = heads[head]
-            if "norms" not in tiles:
-                norms = prep.tile([P, 2 * TILES], F32)
-                tiles["norms"] = norms
+            half_norms = half_norms_tile(head)
             rows = tiles["qk"][:].rearrange("p a j d -> p (a j) d")
             for column in columns:
                 squares = prep.tile([P, FEATURES], BF16)
@@ -106,47 +114,49 @@ def tile_softmaxattention_kde_pa_t_kernel(tc, q_s, k_s, v_s, mask, out):
                     out=squares[:],
                     in_=rows[:, column, :],
                     func=ACT.Square,
-                    accum_out=tiles["norms"][:, column : column + 1],
+                    scale=math.sqrt(0.5),
+                    accum_out=half_norms[:, column : column + 1],
                 )
 
-        def square_sums_by_vector(head, first_column, n_columns):
+        def norm_stats(head, first_column, n_columns):
             tiles = heads[head]
-            if "norms" not in tiles:
-                norms = prep.tile([P, 2 * TILES], F32)
-                tiles["norms"] = norms
             rows = tiles["qk"][:].rearrange("p a j d -> p (a j) d")
-            stats = prep.tile([P, n_columns, 2, 3], F32)
-            for i in range(n_columns):
+            stats = prep.tile([P, n_columns // 2, 2, 3], F32)
+            for i in range(n_columns // 2):
+                column = first_column + 2 * i
                 nc.vector.bn_stats(
-                    out=stats[:, i].rearrange("p e s -> p (e s)"), in_=rows[:, first_column + i, :]
+                    out=stats[:, i].rearrange("p e s -> p (e s)"),
+                    in_=rows[:, column : column + 2, :].rearrange("p e d -> p d e"),
                 )
-            mean_squares = prep.tile([P, n_columns, 2], F32)
-            nc.vector.tensor_tensor(
-                out=mean_squares[:], in0=stats[:, :, :, 1], in1=stats[:, :, :, 1], op=ALU.mult
-            )
-            half_sums = prep.tile([P, n_columns, 2], F32)
+            tiles["stats", first_column] = stats
+
+        def norm_mean_part(head, first_column, n_columns):
+            tiles = heads[head]
+            stats = tiles["stats", first_column]
+            mean_part = prep.tile([P, n_columns // 2, 2], F32)
             nc.vector.scalar_tensor_tensor(
-                out=half_sums[:],
-                in0=mean_squares[:],
-                scalar=float(FEATURES // 2),
-                in1=stats[:, :, :, 2],
+                out=mean_part[:],
+                in0=stats[:, :, :, 1],
+                scalar=0.5 * FEATURES,
+                in1=stats[:, :, :, 1],
+                op0=ALU.mult,
+                op1=ALU.mult,
+            )
+            tiles["mean_part", first_column] = mean_part
+
+        def norm_sum(head, first_column, n_columns):
+            tiles = heads[head]
+            half_norms = half_norms_tile(head)
+            nc.vector.scalar_tensor_tensor(
+                out=half_norms[:, first_column : first_column + n_columns].rearrange(
+                    "p (i e) -> p i e", e=2
+                ),
+                in0=tiles["stats", first_column][:, :, :, 2],
+                scalar=0.5,
+                in1=tiles["mean_part", first_column][:],
                 op0=ALU.mult,
                 op1=ALU.add,
             )
-            nc.vector.tensor_reduce(
-                out=tiles["norms"][:, first_column : first_column + n_columns],
-                in_=half_sums[:],
-                axis=AXIS.X,
-                op=ALU.add,
-            )
-
-        def halve(head):
-            tiles = heads[head]
-            half_norms = prep.tile([P, 2 * TILES], F32)
-            nc.vector.tensor_scalar(
-                out=half_norms[:], in0=tiles["norms"][:], scalar1=0.5, scalar2=None, op0=ALU.mult
-            )
-            tiles["half_norms"] = half_norms
 
         def largest_in_partition(head):
             tiles = heads[head]
@@ -205,10 +215,10 @@ def tile_softmaxattention_kde_pa_t_kernel(tc, q_s, k_s, v_s, mask, out):
                 nc.tensor.transpose(turned_bank[:, j, :], tiles["qk"][:, a, j, :], ident_bf16[:])
             tiles["turned_bank%d" % a] = turned_bank
 
-        def turn_copy(head, a):
+        def turn_copy(head, a, copy=nc.vector.tensor_copy):
             tiles = heads[head]
             turned_sb = prep.tile([P, TILES, P], BF16, name="turned%d" % a)
-            nc.vector.tensor_copy(out=turned_sb[:], in_=tiles["turned_bank%d" % a][:])
+            copy(out=turned_sb[:], in_=tiles["turned_bank%d" % a][:])
             tiles["turned%d" % a] = turned_sb
 
         def v_group(head):
@@ -353,22 +363,36 @@ def tile_softmaxattention_kde_pa_t_kernel(tc, q_s, k_s, v_s, mask, out):
 
         ctx.enter_context(tc.manual_schedule())
 
+        half_tiles = TILES // 2
+        last_q = (half_tiles, half_tiles)
+        last_k = (TILES + half_tiles, half_tiles)
         turn(0, 0)
         turn(0, 1)
-        square_sums(0, range(TILES))
-        square_sums_by_vector(0, TILES, TILES)
-        halve(0)
+        square_sums(0, range(half_tiles))
+        norm_stats(0, *last_q)
+        square_sums(0, range(TILES, TILES + half_tiles))
+        norm_mean_part(0, *last_q)
+        norm_stats(0, *last_k)
+        norm_sum(0, *last_q)
+        norm_mean_part(0, *last_k)
         largest_in_partition(0)
-        turn_copy(0, 0)
         spread_largest(0)
+        turn_copy(0, 0, nc.scalar.copy)
+        turn_copy(0, 1, nc.scalar.copy)
+        norm_sum(0, *last_k)
+        mask_terms()
         largest_of_head(0)
-        turn_copy(0, 1)
         key_bias(0)
-        square_sums(1, range(TILES))
         query_factor(0)
+        square_sums(1, range(half_tiles))
         v_group(0)
-        square_sums_by_vector(1, TILES, TILES)
+        norm_stats(1, *last_q)
+        norm_stats(1, TILES, TILES)
+        norm_mean_part(1, *last_q)
+        norm_mean_part(1, TILES, TILES)
         v_quantize(0)
+        norm_sum(1, *last_q)
+        norm_sum(1, TILES, TILES)
 
         for step in range(n_steps):
             second = step % HALVES == 1
@@ -382,8 +406,6 @@ def tile_softmaxattention_kde_pa_t_kernel(tc, q_s, k_s, v_s, mask, out):
 
             if load_head < n_heads:
                 load(load_head)
-            if turn_head < n_heads:
-                halve(turn_head)
             if last_head < n_heads:
                 key_bias(last_head)
             for tile_index in range(TILES):

@@ -11,7 +11,6 @@ U8 = mybir.dt.uint8
 FP8X4 = mybir.dt.float8_e4m3fn_x4
 ALU = mybir.AluOpType
 ACT = mybir.ActivationFunctionType
-AXIS = mybir.AxisListType
 
 BATCHES, HEADS, TOKENS, FEATURES = 4, 4, 1024, 128
 P = 128
@@ -25,6 +24,8 @@ Q_TILES_PER_HALF = Q_HALF // P
 RUN = 4
 Q_VECTOR = 320
 Q_GPSIMD = Q_HALF - Q_VECTOR
+OUT_LAG = 2
+STATS_FIRST = 10
 MASK_BIAS = 1.0e9
 
 FLOPS = 2 * 2 * BATCHES * HEADS * TOKENS * TOKENS * FEATURES
@@ -36,10 +37,11 @@ def tile_softmaxattention_kde_pa_t_kernel(tc, q_s, k_s, v_s, mask, out):
     n_steps = n_heads * HALVES
     with ExitStack() as ctx:
         const = ctx.enter_context(tc.tile_pool(name="const", bufs=1))
-        inputs = ctx.enter_context(tc.tile_pool(name="inputs", bufs=4))
-        prep = ctx.enter_context(tc.tile_pool(name="prep", bufs=3))
+        inputs = ctx.enter_context(tc.tile_pool(name="inputs", bufs=5))
+        prep = ctx.enter_context(tc.tile_pool(name="prep", bufs=4))
         work = ctx.enter_context(tc.tile_pool(name="work", bufs=3))
         single = ctx.enter_context(tc.tile_pool(name="single", bufs=1))
+        key_parts = ctx.enter_context(tc.tile_pool(name="key_parts", bufs=4))
         score_banks = ctx.enter_context(tc.psum_pool(name="score_banks", bufs=3))
         factor_banks = ctx.enter_context(tc.psum_pool(name="factor_banks", bufs=2))
         out_banks = ctx.enter_context(tc.psum_pool(name="out_banks", bufs=1))
@@ -47,6 +49,8 @@ def tile_softmaxattention_kde_pa_t_kernel(tc, q_s, k_s, v_s, mask, out):
 
         ident_bf16 = const.tile([P, P], BF16)
         make_identity(nc, ident_bf16[:])
+        minus_mean = const.tile([P, P], F32)
+        nc.vector.memset(minus_mean[:], -1.0 / TOKENS)
         ident_f32 = const.tile([P, P], F32)
         make_identity(nc, ident_f32[:])
 
@@ -121,18 +125,18 @@ def tile_softmaxattention_kde_pa_t_kernel(tc, q_s, k_s, v_s, mask, out):
         def norm_stats(head, first_column, n_columns):
             tiles = heads[head]
             rows = tiles["qk"][:].rearrange("p a j d -> p (a j) d")
-            stats = prep.tile([P, n_columns // 2, 2, 3], F32)
-            for i in range(n_columns // 2):
-                column = first_column + 2 * i
+            if "stats" not in tiles:
+                stats = prep.tile([P, TILES, 2, 3], F32)
+                tiles["stats"] = stats
+            for i in range(first_column // 2, (first_column + n_columns) // 2):
                 nc.vector.bn_stats(
-                    out=stats[:, i].rearrange("p e s -> p (e s)"),
-                    in_=rows[:, column : column + 2, :].rearrange("p e d -> p d e"),
+                    out=tiles["stats"][:, i].rearrange("p e s -> p (e s)"),
+                    in_=rows[:, 2 * i : 2 * i + 2, :].rearrange("p e d -> p d e"),
                 )
-            tiles["stats", first_column] = stats
 
         def norm_mean_part(head, first_column, n_columns):
             tiles = heads[head]
-            stats = tiles["stats", first_column]
+            stats = tiles["stats"][:, first_column // 2 : (first_column + n_columns) // 2]
             mean_part = prep.tile([P, n_columns // 2, 2], F32)
             nc.vector.scalar_tensor_tensor(
                 out=mean_part[:],
@@ -151,36 +155,40 @@ def tile_softmaxattention_kde_pa_t_kernel(tc, q_s, k_s, v_s, mask, out):
                 out=half_norms[:, first_column : first_column + n_columns].rearrange(
                     "p (i e) -> p i e", e=2
                 ),
-                in0=tiles["stats", first_column][:, :, :, 2],
+                in0=tiles["stats"][:, first_column // 2 : (first_column + n_columns) // 2, :, 2],
                 scalar=0.5,
                 in1=tiles["mean_part", first_column][:],
                 op0=ALU.mult,
                 op1=ALU.add,
             )
 
-        def largest_in_partition(head):
+        def mean_over_partitions(head):
             tiles = heads[head]
-            largest_of_8 = prep.tile([P, 1], F32)
-            nc.vector.tensor_reduce(
-                out=largest_of_8[:], in_=tiles["half_norms"][:, 0:TILES], axis=AXIS.X, op=ALU.max
+            column_means = turn_banks.tile([P, TILES], F32, tag="turn")
+            nc.tensor.matmul(
+                column_means[:],
+                lhsT=minus_mean[:],
+                rhs=tiles["half_norms"][:, 0:TILES],
+                start=True,
+                stop=True,
             )
-            tiles["largest_of_8"] = largest_of_8
+            tiles["column_means"] = column_means
 
-        def spread_largest(head):
+        def shift_of_head(head):
             tiles = heads[head]
-            spread = turn_banks.tile([P, P], F32, tag="turn")
-            nc.tensor.transpose(
-                spread[:], tiles["largest_of_8"][:, 0:1].to_broadcast([P, P]), ident_f32[:]
-            )
-            tiles["spread_largest"] = spread
-
-        def largest_of_head(head):
-            tiles = heads[head]
+            minus_shift = prep.tile([P, 1], F32)
             shift = prep.tile([P, 1], F32)
-            nc.vector.tensor_reduce(
-                out=shift[:], in_=tiles["spread_largest"][:], axis=AXIS.X, op=ALU.max
-            )
+            for total, scale in ((minus_shift, 1.0), (shift, -1.0)):
+                unused = prep.tile([P, TILES], F32)
+                nc.scalar.activation(
+                    out=unused[:],
+                    in_=tiles["column_means"][:],
+                    func=ACT.Identity,
+                    scale=scale,
+                    accum_out=total[:],
+                )
             tiles["shift"] = shift
+            tiles["minus_shift"] = minus_shift
 
         def query_factor(head):
             tiles = heads[head]
@@ -194,17 +202,27 @@ def tile_softmaxattention_kde_pa_t_kernel(tc, q_s, k_s, v_s, mask, out):
             )
             tiles["q_factor"] = q_factor
 
-        def key_bias(head):
+        def key_term(head):
             tiles = heads[head]
             b = head // HEADS
+            key_terms = prep.tile([P, TILES], F32)
+            nc.vector.tensor_tensor(
+                out=key_terms[:],
+                in0=tiles["half_norms"][:, TILES : 2 * TILES],
+                in1=mask_term[:, b * TILES : (b + 1) * TILES],
+                op=ALU.subtract,
+            )
+            tiles["key_term"] = key_terms
+
+        def key_bias(head):
+            tiles = heads[head]
             bias = prep.tile([P, TILES], F32)
-            nc.vector.scalar_tensor_tensor(
+            nc.scalar.activation(
                 out=bias[:],
-                in0=mask_term[:, b * TILES : (b + 1) * TILES],
-                scalar=tiles["shift"][:, 0:1],
-                in1=tiles["half_norms"][:, TILES : 2 * TILES],
-                op0=ALU.subtract,
-                op1=ALU.subtract,
+                in_=tiles["key_term"][:],
+                func=ACT.Identity,
+                scale=-1.0,
+                bias=tiles["minus_shift"][:, 0:1],
             )
             tiles["key_bias"] = bias
 
@@ -215,10 +233,10 @@ def tile_softmaxattention_kde_pa_t_kernel(tc, q_s, k_s, v_s, mask, out):
                 nc.tensor.transpose(turned_bank[:, j, :], tiles["qk"][:, a, j, :], ident_bf16[:])
             tiles["turned_bank%d" % a] = turned_bank
 
-        def turn_copy(head, a, copy=nc.vector.tensor_copy):
+        def turn_copy(head, a):
             tiles = heads[head]
             turned_sb = prep.tile([P, TILES, P], BF16, name="turned%d" % a)
-            copy(out=turned_sb[:], in_=tiles["turned_bank%d" % a][:])
+            nc.scalar.copy(out=turned_sb[:], in_=tiles["turned_bank%d" % a][:])
             tiles["turned%d" % a] = turned_sb
 
         def v_group(head):
@@ -248,7 +266,7 @@ def tile_softmaxattention_kde_pa_t_kernel(tc, q_s, k_s, v_s, mask, out):
             first = half * Q_TILES_PER_HALF
             c, t = divmod(tile_index, PACK)
             if t == 0:
-                key_part = work.tile([P, PACK, Q_HALF], F32)
+                key_part = key_parts.tile([P, PACK, Q_HALF], F32)
                 steps[step]["key_part%d" % c] = key_part
             score = score_banks.tile([P, Q_HALF], F32)
             nc.tensor.matmul(
@@ -281,12 +299,7 @@ def tile_softmaxattention_kde_pa_t_kernel(tc, q_s, k_s, v_s, mask, out):
 
         def factor_copy(step):
             factor_sb = work.tile([P, Q_GPSIMD], F32)
-            if step % HALVES == 0:
-                nc.scalar.copy(out=factor_sb[:], in_=steps[step]["spread"][:, Q_VECTOR:Q_HALF])
-            else:
-                nc.vector.tensor_copy(
-                    out=factor_sb[:], in_=steps[step]["spread"][:, Q_VECTOR:Q_HALF]
-                )
+            nc.scalar.copy(out=factor_sb[:], in_=steps[step]["spread"][:, Q_VECTOR:Q_HALF])
             steps[step]["factor_sb"] = factor_sb
 
         def multiply(step, c):
@@ -350,7 +363,7 @@ def tile_softmaxattention_kde_pa_t_kernel(tc, q_s, k_s, v_s, mask, out):
             if half == 0:
                 out_rows = prep.tile([P, TILES, FEATURES], F32)
                 heads[head]["out_rows"] = out_rows
-            nc.vector.tensor_copy(
+            nc.scalar.copy(
                 out=heads[head]["out_rows"][:, first : first + Q_TILES_PER_HALF, :],
                 in_=steps[step]["out_sums"][:],
             )
@@ -367,7 +380,6 @@ def tile_softmaxattention_kde_pa_t_kernel(tc, q_s, k_s, v_s, mask, out):
         last_q = (half_tiles, half_tiles)
         last_k = (TILES + half_tiles, half_tiles)
         turn(0, 0)
-        turn(0, 1)
         square_sums(0, range(half_tiles))
         norm_stats(0, *last_q)
         square_sums(0, range(TILES, TILES + half_tiles))
@@ -375,73 +387,69 @@ def tile_softmaxattention_kde_pa_t_kernel(tc, q_s, k_s, v_s, mask, out):
         norm_stats(0, *last_k)
         norm_sum(0, *last_q)
         norm_mean_part(0, *last_k)
-        largest_in_partition(0)
-        spread_largest(0)
-        turn_copy(0, 0, nc.scalar.copy)
-        turn_copy(0, 1, nc.scalar.copy)
-        norm_sum(0, *last_k)
+        turn_copy(0, 0)
+        turn(0, 1)
+        mean_over_partitions(0)
         mask_terms()
-        largest_of_head(0)
+        norm_sum(0, *last_k)
+        turn_copy(0, 1)
+        key_term(0)
+        shift_of_head(0)
         key_bias(0)
         query_factor(0)
-        square_sums(1, range(half_tiles))
-        v_group(0)
-        norm_stats(1, *last_q)
+        norm_stats(1, 0, TILES)
         norm_stats(1, TILES, TILES)
-        norm_mean_part(1, *last_q)
-        norm_mean_part(1, TILES, TILES)
+        norm_mean_part(1, 0, 2 * TILES)
+        v_group(0)
+        norm_sum(1, 0, 2 * TILES)
+        key_term(1)
         v_quantize(0)
-        norm_sum(1, *last_q)
-        norm_sum(1, TILES, TILES)
-
         for step in range(n_steps):
             second = step % HALVES == 1
-            if not second:
-                steps[step] = {}
-                steps[step + 1] = {}
-            squares_head = (step + 3) // HALVES if second else step // HALVES + 2
-            turn_head = n_heads if second else step // HALVES + 1
-            last_head = (step + 1) // HALVES if second else n_heads
-            load_head = n_heads if second else step // HALVES + 3
-
-            if load_head < n_heads:
-                load(load_head)
-            if last_head < n_heads:
-                key_bias(last_head)
+            head = step // HALVES
+            next_head = head + 1
+            stats_head = head + 2
+            steps[step] = {}
+            if not second and head + 3 < n_heads:
+                load(head + 3)
             for tile_index in range(TILES):
                 scores_and_exp(step, tile_index)
-                if squares_head < n_heads:
-                    square_sums(squares_head, [tile_index + (TILES if second else 0)])
-                if tile_index == 0 and not second:
+                if tile_index == 1:
                     spread_factor(step)
+                    if second and next_head < n_heads:
+                        mean_over_partitions(next_head)
+                if tile_index == 2 and next_head < n_heads:
+                    turn(next_head, 1 if second else 0)
+                if tile_index == 4:
                     factor_copy(step)
-                if tile_index == 5 and not second:
-                    spread_factor(step + 1)
-                if tile_index == 2 and turn_head < n_heads:
-                    turn(turn_head, 0)
-                    turn_copy(turn_head, 0)
-                    largest_in_partition(turn_head)
-                if tile_index == 3:
-                    if turn_head < n_heads:
-                        turn(turn_head, 1)
-                    multiply(step, 0)
-                    if turn_head < n_heads:
-                        turn_copy(turn_head, 1)
-                if tile_index == 5 and last_head < n_heads:
-                    query_factor(last_head)
+                    if second and next_head < n_heads:
+                        shift_of_head(next_head)
+                        key_bias(next_head)
+                        query_factor(next_head)
+                if tile_index == 5:
+                    if next_head < n_heads:
+                        turn_copy(next_head, 1 if second else 0)
+                    if step >= OUT_LAG:
+                        attn_times_v(step - OUT_LAG)
+                if tile_index == 7 and step >= OUT_LAG:
+                    out_copy(step - OUT_LAG)
+            multiply(step, 0)
             multiply(step, 1)
-            if not second:
-                factor_copy(step + 1)
-            if step > 0:
-                attn_times_v(step - 1)
-                out_copy(step - 1)
-            if turn_head < n_heads:
-                spread_largest(turn_head)
-                largest_of_head(turn_head)
-            if last_head < n_heads:
-                v_group(last_head)
+            if stats_head < n_heads:
+                if not second:
+                    norm_stats(stats_head, 0, STATS_FIRST)
+                else:
+                    norm_stats(stats_head, STATS_FIRST, 2 * TILES - STATS_FIRST)
+                    norm_mean_part(stats_head, 0, 2 * TILES)
+            if second and next_head < n_heads:
+                v_group(next_head)
+            if second and stats_head < n_heads:
+                norm_sum(stats_head, 0, 2 * TILES)
             quantize(step)
-            if last_head < n_heads:
-                v_quantize(last_head)
-        attn_times_v(n_steps - 1)
-        out_copy(n_steps - 1)
+            if second and next_head < n_heads:
+                v_quantize(next_head)
+            if second and stats_head < n_heads:
+                key_term(stats_head)
+        for step in range(n_steps - OUT_LAG, n_steps):
+            attn_times_v(step)
+            out_copy(step)

@@ -22,10 +22,10 @@ Q_HALF = 512
 HALVES = TOKENS // Q_HALF
 Q_TILES_PER_HALF = Q_HALF // P
 RUN = 4
-Q_VECTOR = 320
+Q_VECTOR = 336
 Q_GPSIMD = Q_HALF - Q_VECTOR
 OUT_LAG = 2
-STATS_FIRST = 10
+STATS_FIRST = 6
 MASK_BIAS = 1.0e9
 
 FLOPS = 2 * 2 * BATCHES * HEADS * TOKENS * TOKENS * FEATURES
@@ -243,7 +243,8 @@ def tile_softmaxattention_kde_pa_t_kernel(tc, q_s, k_s, v_s, mask, out):
             tiles = heads[head]
             v_grouped = prep.tile([P, PASSES, FEATURES, PACK], BF16, align_bytes=64)
             nc.vector.tensor_copy(
-                out=v_grouped[:], in_=tiles["v_rows"][:].rearrange("p c t w -> p c w t")
+                out=v_grouped[:].rearrange("p c (g i) t -> p c g t i", i=RUN),
+                in_=tiles["v_rows"][:].rearrange("p c t (g i) -> p c g t i", i=RUN),
             )
             tiles["v_grouped"] = v_grouped
 
@@ -402,6 +403,7 @@ def tile_softmaxattention_kde_pa_t_kernel(tc, q_s, k_s, v_s, mask, out):
         norm_mean_part(1, 0, 2 * TILES)
         v_group(0)
         norm_sum(1, 0, 2 * TILES)
+        norm_stats(2, 0, STATS_FIRST)
         key_term(1)
         v_quantize(0)
         for step in range(n_steps):
@@ -435,21 +437,25 @@ def tile_softmaxattention_kde_pa_t_kernel(tc, q_s, k_s, v_s, mask, out):
                     out_copy(step - OUT_LAG)
             multiply(step, 0)
             multiply(step, 1)
-            if stats_head < n_heads:
-                if not second:
-                    norm_stats(stats_head, 0, STATS_FIRST)
-                else:
+            if not second:
+                if stats_head < n_heads:
                     norm_stats(stats_head, STATS_FIRST, 2 * TILES - STATS_FIRST)
-                    norm_mean_part(stats_head, 0, 2 * TILES)
-            if second and next_head < n_heads:
-                v_group(next_head)
-            if second and stats_head < n_heads:
-                norm_sum(stats_head, 0, 2 * TILES)
+            else:
+                if stats_head + 1 < n_heads:
+                    norm_stats(stats_head + 1, 0, STATS_FIRST)
+                if next_head < n_heads:
+                    v_group(next_head)
+                if stats_head < n_heads:
+                    norm_sum(stats_head, 0, 2 * TILES)
             quantize(step)
-            if second and next_head < n_heads:
-                v_quantize(next_head)
-            if second and stats_head < n_heads:
-                key_term(stats_head)
+            if not second:
+                if stats_head < n_heads:
+                    norm_mean_part(stats_head, 0, 2 * TILES)
+            else:
+                if next_head < n_heads:
+                    v_quantize(next_head)
+                if stats_head < n_heads:
+                    key_term(stats_head)
         for step in range(n_steps - OUT_LAG, n_steps):
             attn_times_v(step)
             out_copy(step)

@@ -22,10 +22,13 @@ Q_HALF = 512
 HALVES = TOKENS // Q_HALF
 Q_TILES_PER_HALF = Q_HALF // P
 RUN = 4
-Q_VECTOR = 336
-Q_GPSIMD = Q_HALF - Q_VECTOR
+GPSIMD_PASS = 0
+Q_VECTOR = 128
+LAST_STEPS = 5
+Q_VECTOR_LAST = 256
+NORMS_AHEAD = 3
 OUT_LAG = 2
-STATS_FIRST = 6
+STATS_FIRST = 8
 MASK_BIAS = 1.0e9
 
 FLOPS = 2 * 2 * BATCHES * HEADS * TOKENS * TOKENS * FEATURES
@@ -37,7 +40,7 @@ def tile_softmaxattention_kde_pa_t_kernel(tc, q_s, k_s, v_s, mask, out):
     n_steps = n_heads * HALVES
     with ExitStack() as ctx:
         const = ctx.enter_context(tc.tile_pool(name="const", bufs=1))
-        inputs = ctx.enter_context(tc.tile_pool(name="inputs", bufs=5))
+        inputs = ctx.enter_context(tc.tile_pool(name="inputs", bufs=NORMS_AHEAD + 3))
         prep = ctx.enter_context(tc.tile_pool(name="prep", bufs=4))
         work = ctx.enter_context(tc.tile_pool(name="work", bufs=3))
         single = ctx.enter_context(tc.tile_pool(name="single", bufs=1))
@@ -53,6 +56,12 @@ def tile_softmaxattention_kde_pa_t_kernel(tc, q_s, k_s, v_s, mask, out):
         nc.vector.memset(minus_mean[:], -1.0 / TOKENS)
         ident_f32 = const.tile([P, P], F32)
         make_identity(nc, ident_f32[:])
+
+        padded_factors = []
+        for i in range(3):
+            padded = const.tile([P, P], F32, name="padded%d" % i)
+            nc.gpsimd.memset(padded[:], 0.0)
+            padded_factors.append(padded)
 
         mask_rows = const.tile([P, BATCHES * PASSES, PACK], BF16)
         with nc.allow_non_contiguous_dma(reason="the mask is 8 KiB, loaded once, 4 keys a run"):
@@ -89,6 +98,7 @@ def tile_softmaxattention_kde_pa_t_kernel(tc, q_s, k_s, v_s, mask, out):
         load(0)
         load(1)
         load(2)
+        load(3)
 
         def mask_terms():
             nc.vector.tensor_scalar(
@@ -174,30 +184,33 @@ def tile_softmaxattention_kde_pa_t_kernel(tc, q_s, k_s, v_s, mask, out):
             )
             tiles["column_means"] = column_means
 
-        def shift_of_head(head):
+        def exponents(head):
             tiles = heads[head]
             minus_shift = prep.tile([P, 1], F32)
-            shift = prep.tile([P, 1], F32)
-            for total, scale in ((minus_shift, 1.0), (shift, -1.0)):
-                unused = prep.tile([P, TILES], F32)
-                nc.scalar.activation(
-                    out=unused[:],
-                    in_=tiles["column_means"][:],
-                    func=ACT.Identity,
-                    scale=scale,
-                    accum_out=total[:],
-                )
-            tiles["shift"] = shift
-            tiles["minus_shift"] = minus_shift
+            unused = prep.tile([P, TILES], F32)
+            nc.scalar.activation(
+                out=unused[:],
+                in_=tiles["column_means"][:],
+                func=ACT.Identity,
+                accum_out=minus_shift[:],
+            )
+            shifted = prep.tile([P, 2 * TILES], F32)
+            nc.scalar.activation(
+                out=shifted[:],
+                in_=tiles["half_norms"][:],
+                func=ACT.Identity,
+                bias=minus_shift[:, 0:1],
+            )
+            tiles["shifted"] = shifted
+            tiles["key_bias"] = shifted[:, TILES : 2 * TILES]
 
         def query_factor(head):
             tiles = heads[head]
-            q_factor = prep.tile([P, TILES], F32)
+            q_factor = padded_factors[head % len(padded_factors)][:, 0:TILES]
             nc.scalar.activation(
-                out=q_factor[:],
-                in_=tiles["half_norms"][:, 0:TILES],
+                out=q_factor,
+                in_=tiles["shifted"][:, 0:TILES],
                 func=ACT.Exp,
-                bias=tiles["shift"][:, 0:1],
                 scale=-1.0,
             )
             tiles["q_factor"] = q_factor
@@ -205,26 +218,13 @@ def tile_softmaxattention_kde_pa_t_kernel(tc, q_s, k_s, v_s, mask, out):
         def key_term(head):
             tiles = heads[head]
             b = head // HEADS
-            key_terms = prep.tile([P, TILES], F32)
+            key_columns = tiles["half_norms"][:, TILES : 2 * TILES]
             nc.vector.tensor_tensor(
-                out=key_terms[:],
-                in0=tiles["half_norms"][:, TILES : 2 * TILES],
-                in1=mask_term[:, b * TILES : (b + 1) * TILES],
+                out=key_columns,
+                in0=mask_term[:, b * TILES : (b + 1) * TILES],
+                in1=key_columns,
                 op=ALU.subtract,
             )
-            tiles["key_term"] = key_terms
-
-        def key_bias(head):
-            tiles = heads[head]
-            bias = prep.tile([P, TILES], F32)
-            nc.scalar.activation(
-                out=bias[:],
-                in_=tiles["key_term"][:],
-                func=ACT.Identity,
-                scale=-1.0,
-                bias=tiles["minus_shift"][:, 0:1],
-            )
-            tiles["key_bias"] = bias
 
         def turn(head, a):
             tiles = heads[head]
@@ -298,34 +298,52 @@ def tile_softmaxattention_kde_pa_t_kernel(tc, q_s, k_s, v_s, mask, out):
                 )
             steps[step]["spread"] = spread
 
-        def factor_copy(step):
-            factor_sb = work.tile([P, Q_GPSIMD], F32)
-            nc.scalar.copy(out=factor_sb[:], in_=steps[step]["spread"][:, Q_VECTOR:Q_HALF])
-            steps[step]["factor_sb"] = factor_sb
+        def factor_rows(head):
+            turned_factors = turn_banks.tile([P, P], F32, tag="turn")
+            nc.tensor.transpose(
+                turned_factors[:], padded_factors[head % len(padded_factors)][:], ident_f32[:]
+            )
+            heads[head]["turned_factors"] = turned_factors
+
+        def factor_spread(head):
+            b, h = divmod(head, HEADS)
+            rows = prep.tile([TILES, P], F32)
+            nc.scalar.copy(out=rows[:], in_=heads[head]["turned_factors"][0:TILES, :])
+            parked = out[b, h][0:TILES, :]
+            nc.sync.dma_start(out=parked, in_=rows[:])
+            factors = work.tile([P, TOKENS], F32)
+            nc.sync.dma_start(
+                out=factors[:], in_=parked.rearrange("j p -> (j p)").partition_broadcast(P)
+            )
+            heads[head]["factors"] = factors
 
         def multiply(step, c):
+            head, half = divmod(step, HALVES)
             tiles = steps[step]
             if c == 0:
                 attn = single.tile([P, PASSES, Q_HALF, PACK], BF16, align_bytes=64)
                 tiles["attn"] = attn
             attn = tiles["attn"]
             key_part = tiles["key_part%d" % c]
-            nc.gpsimd.tensor_tensor(
-                out=attn[:, c, Q_VECTOR:Q_HALF, :].rearrange("p (g i) t -> p g t i", i=RUN),
-                in0=key_part[:, :, Q_VECTOR:Q_HALF].rearrange("p t (g i) -> p g t i", i=RUN),
-                in1=tiles["factor_sb"][:]
-                .rearrange("p (g i) -> p g i", i=RUN)
-                .unsqueeze(2)
-                .to_broadcast([P, Q_GPSIMD // RUN, PACK, RUN]),
-                op=ALU.mult,
-            )
+            split = Q_HALF
+            if c == GPSIMD_PASS:
+                split = Q_VECTOR if step < n_steps - LAST_STEPS else Q_VECTOR_LAST
+                nc.gpsimd.tensor_tensor(
+                    out=attn[:, c, split:Q_HALF, :].rearrange("p (g i) t -> p g t i", i=RUN),
+                    in0=key_part[:, :, split:Q_HALF].rearrange("p t (g i) -> p g t i", i=RUN),
+                    in1=heads[head]["factors"][:, half * Q_HALF + split : (half + 1) * Q_HALF]
+                    .rearrange("p (g i) -> p g i", i=RUN)
+                    .unsqueeze(2)
+                    .to_broadcast([P, (Q_HALF - split) // RUN, PACK, RUN]),
+                    op=ALU.mult,
+                )
             nc.vector.tensor_tensor(
-                out=attn[:, c, 0:Q_VECTOR, :].rearrange("p (g i) t -> p g t i", i=RUN),
-                in0=key_part[:, :, 0:Q_VECTOR].rearrange("p t (g i) -> p g t i", i=RUN),
-                in1=tiles["spread"][:, 0:Q_VECTOR]
+                out=attn[:, c, 0:split, :].rearrange("p (g i) t -> p g t i", i=RUN),
+                in0=key_part[:, :, 0:split].rearrange("p t (g i) -> p g t i", i=RUN),
+                in1=tiles["spread"][:, 0:split]
                 .rearrange("p (g i) -> p g i", i=RUN)
                 .unsqueeze(2)
-                .to_broadcast([P, Q_VECTOR // RUN, PACK, RUN]),
+                .to_broadcast([P, split // RUN, PACK, RUN]),
                 op=ALU.mult,
             )
 
@@ -368,7 +386,13 @@ def tile_softmaxattention_kde_pa_t_kernel(tc, q_s, k_s, v_s, mask, out):
                 out=heads[head]["out_rows"][:, first : first + Q_TILES_PER_HALF, :],
                 in_=steps[step]["out_sums"][:],
             )
-            if half == HALVES - 1:
+            if head == n_heads - 1:
+                b, h = divmod(head, HEADS)
+                nc.sync.dma_start(
+                    out=out[b, h].rearrange("(p j) f -> p j f", j=TILES)[:, first : first + Q_TILES_PER_HALF],
+                    in_=heads[head]["out_rows"][:, first : first + Q_TILES_PER_HALF],
+                )
+            elif half == HALVES - 1:
                 b, h = divmod(head, HEADS)
                 nc.sync.dma_start(
                     out=out[b, h].rearrange("(p j) f -> p j f", j=TILES),
@@ -380,6 +404,7 @@ def tile_softmaxattention_kde_pa_t_kernel(tc, q_s, k_s, v_s, mask, out):
         half_tiles = TILES // 2
         last_q = (half_tiles, half_tiles)
         last_k = (TILES + half_tiles, half_tiles)
+        whole = (0, 2 * TILES)
         turn(0, 0)
         square_sums(0, range(half_tiles))
         norm_stats(0, *last_q)
@@ -395,67 +420,73 @@ def tile_softmaxattention_kde_pa_t_kernel(tc, q_s, k_s, v_s, mask, out):
         norm_sum(0, *last_k)
         turn_copy(0, 1)
         key_term(0)
-        shift_of_head(0)
-        key_bias(0)
+        exponents(0)
         query_factor(0)
-        norm_stats(1, 0, TILES)
-        norm_stats(1, TILES, TILES)
-        norm_mean_part(1, 0, 2 * TILES)
+        factor_rows(0)
+        factor_spread(0)
+        norm_stats(1, *whole)
         v_group(0)
-        norm_sum(1, 0, 2 * TILES)
-        norm_stats(2, 0, STATS_FIRST)
-        key_term(1)
+        norm_mean_part(1, *whole)
         v_quantize(0)
+        norm_sum(1, *whole)
+        norm_stats(2, *whole)
+        key_term(1)
+        norm_mean_part(2, *whole)
+        norm_stats(NORMS_AHEAD, 0, STATS_FIRST)
+        norm_sum(2, *whole)
+        key_term(2)
+
         for step in range(n_steps):
             second = step % HALVES == 1
             head = step // HALVES
             next_head = head + 1
-            stats_head = head + 2
+            norms_head = head + NORMS_AHEAD
             steps[step] = {}
-            if not second and head + 3 < n_heads:
-                load(head + 3)
+            if not second and norms_head + 1 < n_heads:
+                load(norms_head + 1)
             for tile_index in range(TILES):
                 scores_and_exp(step, tile_index)
+                if next_head < n_heads:
+                    if not second and tile_index == 4:
+                        mean_over_partitions(next_head)
+                    if not second and tile_index == 7:
+                        exponents(next_head)
+                        query_factor(next_head)
+                    if second and tile_index == 1:
+                        factor_rows(next_head)
+                    if second and tile_index == 3:
+                        factor_spread(next_head)
+                    if tile_index == 2:
+                        turn(next_head, 1 if second else 0)
+                    if tile_index == 5:
+                        turn_copy(next_head, 1 if second else 0)
                 if tile_index == 1:
                     spread_factor(step)
-                    if second and next_head < n_heads:
-                        mean_over_partitions(next_head)
-                if tile_index == 2 and next_head < n_heads:
-                    turn(next_head, 1 if second else 0)
-                if tile_index == 4:
-                    factor_copy(step)
-                    if second and next_head < n_heads:
-                        shift_of_head(next_head)
-                        key_bias(next_head)
-                        query_factor(next_head)
-                if tile_index == 5:
-                    if next_head < n_heads:
-                        turn_copy(next_head, 1 if second else 0)
-                    if step >= OUT_LAG:
-                        attn_times_v(step - OUT_LAG)
+                if tile_index == 5 and step >= OUT_LAG:
+                    attn_times_v(step - OUT_LAG)
                 if tile_index == 7 and step >= OUT_LAG:
                     out_copy(step - OUT_LAG)
             multiply(step, 0)
             multiply(step, 1)
             if not second:
-                if stats_head < n_heads:
-                    norm_stats(stats_head, STATS_FIRST, 2 * TILES - STATS_FIRST)
+                if norms_head < n_heads:
+                    norm_stats(norms_head, STATS_FIRST, 2 * TILES - STATS_FIRST)
             else:
-                if stats_head + 1 < n_heads:
-                    norm_stats(stats_head + 1, 0, STATS_FIRST)
+                if norms_head + 1 < n_heads:
+                    norm_stats(norms_head + 1, 0, STATS_FIRST)
                 if next_head < n_heads:
                     v_group(next_head)
-                if stats_head < n_heads:
-                    norm_sum(stats_head, 0, 2 * TILES)
+                if norms_head < n_heads:
+                    norm_sum(norms_head, *whole)
             quantize(step)
             if not second:
-                if stats_head < n_heads:
-                    norm_mean_part(stats_head, 0, 2 * TILES)
+                if norms_head < n_heads:
+                    norm_mean_part(norms_head, *whole)
             else:
                 if next_head < n_heads:
                     v_quantize(next_head)
-                if stats_head < n_heads:
-                    key_term(stats_head)
+                if norms_head < n_heads:
+                    key_term(norms_head)
         for step in range(n_steps - OUT_LAG, n_steps):
             attn_times_v(step)
             out_copy(step)

@@ -184,7 +184,7 @@ def tile_softmaxattention_kde_pa_t_kernel(tc, q_s, k_s, v_s, mask, out):
             )
             tiles["column_means"] = column_means
 
-        def exponents(head):
+        def sum_shift(head):
             tiles = heads[head]
             minus_shift = prep.tile([P, 1], F32)
             unused = prep.tile([P, TILES], F32)
@@ -194,12 +194,16 @@ def tile_softmaxattention_kde_pa_t_kernel(tc, q_s, k_s, v_s, mask, out):
                 func=ACT.Identity,
                 accum_out=minus_shift[:],
             )
+            tiles["minus_shift"] = minus_shift
+
+        def exponents(head):
+            tiles = heads[head]
             shifted = prep.tile([P, 2 * TILES], F32)
             nc.scalar.activation(
                 out=shifted[:],
                 in_=tiles["half_norms"][:],
                 func=ACT.Identity,
-                bias=minus_shift[:, 0:1],
+                bias=tiles["minus_shift"][:, 0:1],
             )
             tiles["shifted"] = shifted
             tiles["key_bias"] = shifted[:, TILES : 2 * TILES]
@@ -420,6 +424,7 @@ def tile_softmaxattention_kde_pa_t_kernel(tc, q_s, k_s, v_s, mask, out):
         norm_sum(0, *last_k)
         turn_copy(0, 1)
         key_term(0)
+        sum_shift(0)
         exponents(0)
         query_factor(0)
         factor_rows(0)
@@ -436,6 +441,19 @@ def tile_softmaxattention_kde_pa_t_kernel(tc, q_s, k_s, v_s, mask, out):
         norm_sum(2, *whole)
         key_term(2)
 
+        chain = {}
+        for head in range(1, n_heads):
+            start = (HALVES * head - 3) * TILES + 5 if head > 1 else 3
+            for offset, stage in (
+                (0, mean_over_partitions),
+                (2, sum_shift),
+                (3, exponents),
+                (4, query_factor),
+                (7, factor_rows),
+                (9, factor_spread),
+            ):
+                chain.setdefault(start + offset, []).append((stage, head))
+
         for step in range(n_steps):
             second = step % HALVES == 1
             head = step // HALVES
@@ -446,16 +464,9 @@ def tile_softmaxattention_kde_pa_t_kernel(tc, q_s, k_s, v_s, mask, out):
                 load(norms_head + 1)
             for tile_index in range(TILES):
                 scores_and_exp(step, tile_index)
+                for stage, chain_head in chain.get(step * TILES + tile_index, []):
+                    stage(chain_head)
                 if next_head < n_heads:
-                    if not second and tile_index == 4:
-                        mean_over_partitions(next_head)
-                    if not second and tile_index == 7:
-                        exponents(next_head)
-                        query_factor(next_head)
-                    if second and tile_index == 1:
-                        factor_rows(next_head)
-                    if second and tile_index == 3:
-                        factor_spread(next_head)
                     if tile_index == 2:
                         turn(next_head, 1 if second else 0)
                     if tile_index == 5:

@@ -26,6 +26,8 @@ GPSIMD_PASS = 0
 Q_VECTOR = 128
 LAST_STEPS = 5
 Q_VECTOR_LAST = 256
+FIRST_HEADS = 2
+Q_VECTOR_FIRST = 336
 NORMS_AHEAD = 3
 OUT_LAG = 2
 STATS_FIRST = 8
@@ -315,11 +317,21 @@ def tile_softmaxattention_kde_pa_t_kernel(tc, q_s, k_s, v_s, mask, out):
             nc.scalar.copy(out=rows[:], in_=heads[head]["turned_factors"][0:TILES, :])
             parked = out[b, h][0:TILES, :]
             nc.sync.dma_start(out=parked, in_=rows[:])
-            factors = work.tile([P, TOKENS], F32)
-            nc.sync.dma_start(
-                out=factors[:], in_=parked.rearrange("j p -> (j p)").partition_broadcast(P)
-            )
-            heads[head]["factors"] = factors
+            for half in range(HALVES):
+                first = half * Q_TILES_PER_HALF
+                factors = work.tile([P, Q_HALF - Q_VECTOR], F32, name="factors%d" % half)
+                nc.sync.dma_start(
+                    out=factors[:],
+                    in_=parked[first : first + Q_TILES_PER_HALF, :]
+                    .rearrange("j p -> (j p)")[Q_VECTOR:Q_HALF]
+                    .partition_broadcast(P),
+                )
+                heads[head]["factors%d" % half] = factors
+
+        def factor_copy(step):
+            factors = work.tile([P, Q_HALF - Q_VECTOR_FIRST], F32)
+            nc.scalar.copy(out=factors[:], in_=steps[step]["spread"][:, Q_VECTOR_FIRST:Q_HALF])
+            steps[step]["factors"] = factors
 
         def multiply(step, c):
             head, half = divmod(step, HALVES)
@@ -329,14 +341,19 @@ def tile_softmaxattention_kde_pa_t_kernel(tc, q_s, k_s, v_s, mask, out):
                 tiles["attn"] = attn
             attn = tiles["attn"]
             key_part = tiles["key_part%d" % c]
-            split = Q_HALF
-            if c == GPSIMD_PASS:
+            if head < FIRST_HEADS:
+                split = Q_VECTOR_FIRST
+                factors = tiles["factors"][:]
+            elif c == GPSIMD_PASS:
                 split = Q_VECTOR if step < n_steps - LAST_STEPS else Q_VECTOR_LAST
+                factors = heads[head]["factors%d" % half][:, split - Q_VECTOR :]
+            else:
+                split = Q_HALF
+            if split < Q_HALF:
                 nc.gpsimd.tensor_tensor(
                     out=attn[:, c, split:Q_HALF, :].rearrange("p (g i) t -> p g t i", i=RUN),
                     in0=key_part[:, :, split:Q_HALF].rearrange("p t (g i) -> p g t i", i=RUN),
-                    in1=heads[head]["factors"][:, half * Q_HALF + split : (half + 1) * Q_HALF]
-                    .rearrange("p (g i) -> p g i", i=RUN)
+                    in1=factors.rearrange("p (g i) -> p g i", i=RUN)
                     .unsqueeze(2)
                     .to_broadcast([P, (Q_HALF - split) // RUN, PACK, RUN]),
                     op=ALU.mult,
@@ -386,7 +403,8 @@ def tile_softmaxattention_kde_pa_t_kernel(tc, q_s, k_s, v_s, mask, out):
             if half == 0:
                 out_rows = prep.tile([P, TILES, FEATURES], F32)
                 heads[head]["out_rows"] = out_rows
-            nc.scalar.copy(
+            copy = nc.vector.tensor_copy if step % 4 == 3 else nc.scalar.copy
+            copy(
                 out=heads[head]["out_rows"][:, first : first + Q_TILES_PER_HALF, :],
                 in_=steps[step]["out_sums"][:],
             )
@@ -427,8 +445,6 @@ def tile_softmaxattention_kde_pa_t_kernel(tc, q_s, k_s, v_s, mask, out):
         sum_shift(0)
         exponents(0)
         query_factor(0)
-        factor_rows(0)
-        factor_spread(0)
         norm_stats(1, *whole)
         v_group(0)
         norm_mean_part(1, *whole)
@@ -443,15 +459,16 @@ def tile_softmaxattention_kde_pa_t_kernel(tc, q_s, k_s, v_s, mask, out):
 
         chain = {}
         for head in range(1, n_heads):
-            start = (HALVES * head - 3) * TILES + 5 if head > 1 else 3
-            for offset, stage in (
+            start = max((HALVES * head - 3) * TILES + 1, 3)
+            stages = [
                 (0, mean_over_partitions),
                 (2, sum_shift),
                 (3, exponents),
                 (4, query_factor),
-                (7, factor_rows),
-                (9, factor_spread),
-            ):
+            ]
+            if head >= FIRST_HEADS:
+                stages += [(7, factor_rows), (9, factor_spread)]
+            for offset, stage in stages:
                 chain.setdefault(start + offset, []).append((stage, head))
 
         for step in range(n_steps):
@@ -473,6 +490,8 @@ def tile_softmaxattention_kde_pa_t_kernel(tc, q_s, k_s, v_s, mask, out):
                         turn_copy(next_head, 1 if second else 0)
                 if tile_index == 1:
                     spread_factor(step)
+                if tile_index == 4 and head < FIRST_HEADS:
+                    factor_copy(step)
                 if tile_index == 5 and step >= OUT_LAG:
                     attn_times_v(step - OUT_LAG)
                 if tile_index == 7 and step >= OUT_LAG:

@@ -23,7 +23,7 @@ HALVES = TOKENS // Q_HALF
 Q_TILES_PER_HALF = Q_HALF // P
 RUN = 4
 GPSIMD_PASS = 0
-Q_VECTOR = 128
+Q_VECTOR = 96
 LAST_STEPS = 5
 Q_VECTOR_LAST = 256
 FIRST_HEADS = 2
@@ -403,8 +403,7 @@ def tile_softmaxattention_kde_pa_t_kernel(tc, q_s, k_s, v_s, mask, out):
             if half == 0:
                 out_rows = prep.tile([P, TILES, FEATURES], F32)
                 heads[head]["out_rows"] = out_rows
-            copy = nc.vector.tensor_copy if step % 4 == 3 else nc.scalar.copy
-            copy(
+            nc.scalar.copy(
                 out=heads[head]["out_rows"][:, first : first + Q_TILES_PER_HALF, :],
                 in_=steps[step]["out_sums"][:],
             )
@@ -459,7 +458,7 @@ def tile_softmaxattention_kde_pa_t_kernel(tc, q_s, k_s, v_s, mask, out):
 
         chain = {}
         for head in range(1, n_heads):
-            start = max((HALVES * head - 3) * TILES + 1, 3)
+            start = max((HALVES * head - 3) * TILES + 4, 3)
             stages = [
                 (0, mean_over_partitions),
                 (2, sum_shift),

@@ -23,9 +23,9 @@ HALVES = TOKENS // Q_HALF
 Q_TILES_PER_HALF = Q_HALF // P
 RUN = 4
 GPSIMD_PASS = 0
-Q_VECTOR = 96
+Q_VECTOR = 80
 LAST_STEPS = 5
-Q_VECTOR_LAST = 256
+Q_VECTOR_LAST = 224
 FIRST_HEADS = 2
 Q_VECTOR_FIRST = 336
 NORMS_AHEAD = 3
@@ -176,7 +176,10 @@ def tile_softmaxattention_kde_pa_t_kernel(tc, q_s, k_s, v_s, mask, out):
 
         def mean_over_partitions(head):
             tiles = heads[head]
-            column_means = turn_banks.tile([P, TILES], F32, tag="turn")
+            if head == 0:
+                column_means = out_banks.tile([P, TILES], F32, tag="out")
+            else:
+                column_means = turn_banks.tile([P, TILES], F32, tag="turn")
             nc.tensor.matmul(
                 column_means[:],
                 lhsT=minus_mean[:],
@@ -245,14 +248,15 @@ def tile_softmaxattention_kde_pa_t_kernel(tc, q_s, k_s, v_s, mask, out):
             nc.scalar.copy(out=turned_sb[:], in_=tiles["turned_bank%d" % a][:])
             tiles["turned%d" % a] = turned_sb
 
-        def v_group(head):
+        def v_group(head, c):
             tiles = heads[head]
-            v_grouped = prep.tile([P, PASSES, FEATURES, PACK], BF16, align_bytes=64)
+            if c == 0:
+                v_grouped = prep.tile([P, PASSES, FEATURES, PACK], BF16, align_bytes=64)
+                tiles["v_grouped"] = v_grouped
             nc.vector.tensor_copy(
-                out=v_grouped[:].rearrange("p c (g i) t -> p c g t i", i=RUN),
-                in_=tiles["v_rows"][:].rearrange("p c t (g i) -> p c g t i", i=RUN),
+                out=tiles["v_grouped"][:, c].rearrange("p (g i) t -> p g t i", i=RUN),
+                in_=tiles["v_rows"][:, c].rearrange("p t (g i) -> p g t i", i=RUN),
             )
-            tiles["v_grouped"] = v_grouped
 
         def v_quantize(head):
             tiles = heads[head]
@@ -380,45 +384,44 @@ def tile_softmaxattention_kde_pa_t_kernel(tc, q_s, k_s, v_s, mask, out):
             tiles["attn_codes"] = attn_codes
             tiles["attn_scales"] = attn_scales
 
-        def attn_times_v(step):
+        def attn_times_v(step, first=0, n=Q_TILES_PER_HALF):
             head = step // HALVES
             tiles = steps[step]
-            out_sums = out_banks.tile([P, Q_TILES_PER_HALF, FEATURES], F32)
-            for i in range(Q_TILES_PER_HALF):
+            if first == 0:
+                out_sums = out_banks.tile([P, n, FEATURES], F32, tag="out")
+            else:
+                out_sums = turn_banks.tile([P, n, FEATURES], F32, tag="turn")
+            for i in range(n):
+                queries = slice((first + i) * P, (first + i + 1) * P)
                 for c in range(PASSES):
                     nc.tensor.matmul_mx(
                         out=out_sums[:, i, :],
-                        lhsT=tiles["attn_codes"][:, c, i * P : (i + 1) * P].bitcast(FP8X4),
-                        lhsT_scale=tiles["attn_scales"][:, c, i * P : (i + 1) * P],
+                        lhsT=tiles["attn_codes"][:, c, queries].bitcast(FP8X4),
+                        lhsT_scale=tiles["attn_scales"][:, c, queries],
                         rhs=heads[head]["v_codes"][:, c, :].bitcast(FP8X4),
                         rhs_scale=heads[head]["v_scales"][:, c, :],
                         start=(c == 0),
                         stop=(c == PASSES - 1),
                     )
-            tiles["out_sums"] = out_sums
+            tiles["out_sums%d" % first] = out_sums
 
-        def out_copy(step):
+        def out_copy(step, copy, first=0, n=Q_TILES_PER_HALF):
             head, half = divmod(step, HALVES)
-            first = half * Q_TILES_PER_HALF
-            if half == 0:
+            if "out_rows" not in heads[head]:
                 out_rows = prep.tile([P, TILES, FEATURES], F32)
                 heads[head]["out_rows"] = out_rows
-            nc.scalar.copy(
-                out=heads[head]["out_rows"][:, first : first + Q_TILES_PER_HALF, :],
-                in_=steps[step]["out_sums"][:],
+            start = half * Q_TILES_PER_HALF + first
+            copy(
+                out=heads[head]["out_rows"][:, start : start + n, :],
+                in_=steps[step]["out_sums%d" % first][:],
             )
-            if head == n_heads - 1:
-                b, h = divmod(head, HEADS)
-                nc.sync.dma_start(
-                    out=out[b, h].rearrange("(p j) f -> p j f", j=TILES)[:, first : first + Q_TILES_PER_HALF],
-                    in_=heads[head]["out_rows"][:, first : first + Q_TILES_PER_HALF],
-                )
-            elif half == HALVES - 1:
-                b, h = divmod(head, HEADS)
-                nc.sync.dma_start(
-                    out=out[b, h].rearrange("(p j) f -> p j f", j=TILES),
-                    in_=heads[head]["out_rows"][:],
-                )
+
+        def store(head, first, n):
+            b, h = divmod(head, HEADS)
+            nc.sync.dma_start(
+                out=out[b, h].rearrange("(p j) f -> p j f", j=TILES)[:, first : first + n],
+                in_=heads[head]["out_rows"][:, first : first + n],
+            )
 
         ctx.enter_context(tc.manual_schedule())
 
@@ -427,6 +430,7 @@ def tile_softmaxattention_kde_pa_t_kernel(tc, q_s, k_s, v_s, mask, out):
         last_k = (TILES + half_tiles, half_tiles)
         whole = (0, 2 * TILES)
         turn(0, 0)
+        turn(0, 1)
         square_sums(0, range(half_tiles))
         norm_stats(0, *last_q)
         square_sums(0, range(TILES, TILES + half_tiles))
@@ -435,17 +439,17 @@ def tile_softmaxattention_kde_pa_t_kernel(tc, q_s, k_s, v_s, mask, out):
         norm_sum(0, *last_q)
         norm_mean_part(0, *last_k)
         turn_copy(0, 0)
-        turn(0, 1)
         mean_over_partitions(0)
         mask_terms()
         norm_sum(0, *last_k)
+        sum_shift(0)
         turn_copy(0, 1)
         key_term(0)
-        sum_shift(0)
         exponents(0)
         query_factor(0)
         norm_stats(1, *whole)
-        v_group(0)
+        v_group(0, 0)
+        v_group(0, 1)
         norm_mean_part(1, *whole)
         v_quantize(0)
         norm_sum(1, *whole)
@@ -494,17 +498,22 @@ def tile_softmaxattention_kde_pa_t_kernel(tc, q_s, k_s, v_s, mask, out):
                 if tile_index == 5 and step >= OUT_LAG:
                     attn_times_v(step - OUT_LAG)
                 if tile_index == 7 and step >= OUT_LAG:
-                    out_copy(step - OUT_LAG)
+                    done = step - OUT_LAG
+                    out_copy(done, nc.scalar.copy)
+                    if done % HALVES == HALVES - 1:
+                        store(done // HALVES, 0, TILES)
             multiply(step, 0)
             multiply(step, 1)
             if not second:
                 if norms_head < n_heads:
                     norm_stats(norms_head, STATS_FIRST, 2 * TILES - STATS_FIRST)
+                if next_head < n_heads:
+                    v_group(next_head, 0)
             else:
                 if norms_head + 1 < n_heads:
                     norm_stats(norms_head + 1, 0, STATS_FIRST)
                 if next_head < n_heads:
-                    v_group(next_head)
+                    v_group(next_head, 1)
                 if norms_head < n_heads:
                     norm_sum(norms_head, *whole)
             quantize(step)
@@ -516,6 +525,11 @@ def tile_softmaxattention_kde_pa_t_kernel(tc, q_s, k_s, v_s, mask, out):
                     v_quantize(next_head)
                 if norms_head < n_heads:
                     key_term(norms_head)
-        for step in range(n_steps - OUT_LAG, n_steps):
-            attn_times_v(step)
-            out_copy(step)
+        attn_times_v(n_steps - 2)
+        out_copy(n_steps - 2, nc.scalar.copy)
+        store(n_heads - 1, 0, Q_TILES_PER_HALF)
+        pair = Q_TILES_PER_HALF // 2
+        for first, copy in ((0, nc.scalar.copy), (pair, nc.vector.tensor_copy)):
+            attn_times_v(n_steps - 1, first, pair)
+            out_copy(n_steps - 1, copy, first, pair)
+            store(n_heads - 1, Q_TILES_PER_HALF + first, pair)

import math
from contextlib import ExitStack

import concourse.mybir as mybir
from concourse.masks import make_identity

BF16 = mybir.dt.bfloat16
F32 = mybir.dt.float32
U32 = mybir.dt.uint32
U8 = mybir.dt.uint8
FP8X4 = mybir.dt.float8_e4m3fn_x4
ALU = mybir.AluOpType
ACT = mybir.ActivationFunctionType

BATCHES, HEADS, TOKENS, FEATURES = 4, 4, 1024, 128
P = 128
PACK = 4
K_PASS = P * PACK
PASSES = TOKENS // K_PASS
TILES = TOKENS // P
Q_HALF = 512
HALVES = TOKENS // Q_HALF
Q_TILES_PER_HALF = Q_HALF // P
RUN = 4
GPSIMD_PASS = 0
Q_VECTOR = 80
LAST_STEPS = 5
Q_VECTOR_LAST = 224
FIRST_HEADS = 2
Q_VECTOR_FIRST = 336
NORMS_AHEAD = 3
OUT_LAG = 2
STATS_FIRST = 8
MASK_BIAS = 1.0e9

FLOPS = 2 * 2 * BATCHES * HEADS * TOKENS * TOKENS * FEATURES


def tile_softmaxattention_kde_pa_t_kernel(tc, q_s, k_s, v_s, mask, out):
    nc = tc.nc
    n_heads = BATCHES * HEADS
    n_steps = n_heads * HALVES
    with ExitStack() as ctx:
        const = ctx.enter_context(tc.tile_pool(name="const", bufs=1))
        inputs = ctx.enter_context(tc.tile_pool(name="inputs", bufs=NORMS_AHEAD + 3))
        prep = ctx.enter_context(tc.tile_pool(name="prep", bufs=4))
        work = ctx.enter_context(tc.tile_pool(name="work", bufs=3))
        single = ctx.enter_context(tc.tile_pool(name="single", bufs=1))
        key_parts = ctx.enter_context(tc.tile_pool(name="key_parts", bufs=4))
        score_banks = ctx.enter_context(tc.psum_pool(name="score_banks", bufs=3))
        factor_banks = ctx.enter_context(tc.psum_pool(name="factor_banks", bufs=2))
        out_banks = ctx.enter_context(tc.psum_pool(name="out_banks", bufs=1))
        turn_banks = ctx.enter_context(tc.psum_pool(name="turn_banks", bufs=2))

        ident_bf16 = const.tile([P, P], BF16)
        make_identity(nc, ident_bf16[:])
        minus_mean = const.tile([P, P], F32)
        nc.vector.memset(minus_mean[:], -1.0 / TOKENS)
        ident_f32 = const.tile([P, P], F32)
        make_identity(nc, ident_f32[:])

        padded_factors = []
        for i in range(3):
            padded = const.tile([P, P], F32, name="padded%d" % i)
            nc.gpsimd.memset(padded[:], 0.0)
            padded_factors.append(padded)

        mask_rows = const.tile([P, BATCHES * PASSES, PACK], BF16)
        with nc.allow_non_contiguous_dma(reason="the mask is 8 KiB, loaded once, 4 keys a run"):
            nc.scalar.dma_start(
                out=mask_rows[:],
                in_=mask.rearrange("b (c p t) -> p (b c) t", c=PASSES, t=PACK),
            )
        mask_term = const.tile([P, BATCHES * TILES], F32)

        warm = const.tile([P, 1], F32)
        nc.vector.memset(warm[:], 0.0)
        nc.scalar.activation(out=warm[:], in_=warm[:], func=ACT.Exp)

        heads = {}
        steps = {}

        def load(head):
            b, h = divmod(head, HEADS)
            qk = inputs.tile([P, 2, TILES, FEATURES], BF16)
            nc.sync.dma_start(
                out=qk[:, 0], in_=q_s[b, h].rearrange("(p j) d -> p j d", j=TILES)
            )
            nc.sync.dma_start(
                out=qk[:, 1].rearrange("p (c t) d -> p c t d", c=PASSES),
                in_=k_s[b, h].rearrange("(c p t) d -> p c t d", c=PASSES, t=PACK),
            )
            v_rows = inputs.tile([P, PASSES, PACK, FEATURES], BF16)
            nc.sync.dma_start(
                out=v_rows[:],
                in_=v_s[b, h].rearrange("(c p t) d -> p c t d", c=PASSES, t=PACK),
            )
            heads[head] = {"qk": qk, "v_rows": v_rows}

        load(0)
        load(1)
        load(2)
        load(3)

        def mask_terms():
            nc.vector.tensor_scalar(
                out=mask_term[:],
                in0=mask_rows[:].rearrange("p a t -> p (a t)"),
                scalar1=MASK_BIAS,
                scalar2=-MASK_BIAS,
                op0=ALU.mult,
                op1=ALU.add,
            )


        def half_norms_tile(head):
            tiles = heads[head]
            if "half_norms" not in tiles:
                half_norms = prep.tile([P, 2 * TILES], F32)
                tiles["half_norms"] = half_norms
            return tiles["half_norms"]

        def square_sums(head, columns):
            tiles = heads[head]
            half_norms = half_norms_tile(head)
            rows = tiles["qk"][:].rearrange("p a j d -> p (a j) d")
            for column in columns:
                squares = prep.tile([P, FEATURES], BF16)
                nc.scalar.activation(
                    out=squares[:],
                    in_=rows[:, column, :],
                    func=ACT.Square,
                    scale=math.sqrt(0.5),
                    accum_out=half_norms[:, column : column + 1],
                )

        def norm_stats(head, first_column, n_columns):
            tiles = heads[head]
            rows = tiles["qk"][:].rearrange("p a j d -> p (a j) d")
            if "stats" not in tiles:
                stats = prep.tile([P, TILES, 2, 3], F32)
                tiles["stats"] = stats
            for i in range(first_column // 2, (first_column + n_columns) // 2):
                nc.vector.bn_stats(
                    out=tiles["stats"][:, i].rearrange("p e s -> p (e s)"),
                    in_=rows[:, 2 * i : 2 * i + 2, :].rearrange("p e d -> p d e"),
                )

        def norm_mean_part(head, first_column, n_columns):
            tiles = heads[head]
            stats = tiles["stats"][:, first_column // 2 : (first_column + n_columns) // 2]
            mean_part = prep.tile([P, n_columns // 2, 2], F32)
            nc.vector.scalar_tensor_tensor(
                out=mean_part[:],
                in0=stats[:, :, :, 1],
                scalar=0.5 * FEATURES,
                in1=stats[:, :, :, 1],
                op0=ALU.mult,
                op1=ALU.mult,
            )
            tiles["mean_part", first_column] = mean_part

        def norm_sum(head, first_column, n_columns):
            tiles = heads[head]
            half_norms = half_norms_tile(head)
            nc.vector.scalar_tensor_tensor(
                out=half_norms[:, first_column : first_column + n_columns].rearrange(
                    "p (i e) -> p i e", e=2
                ),
                in0=tiles["stats"][:, first_column // 2 : (first_column + n_columns) // 2, :, 2],
                scalar=0.5,
                in1=tiles["mean_part", first_column][:],
                op0=ALU.mult,
                op1=ALU.add,
            )

        def mean_over_partitions(head):
            tiles = heads[head]
            if head == 0:
                column_means = out_banks.tile([P, TILES], F32, tag="out")
            else:
                column_means = turn_banks.tile([P, TILES], F32, tag="turn")
            nc.tensor.matmul(
                column_means[:],
                lhsT=minus_mean[:],
                rhs=tiles["half_norms"][:, 0:TILES],
                start=True,
                stop=True,
            )
            tiles["column_means"] = column_means

        def sum_shift(head):
            tiles = heads[head]
            minus_shift = prep.tile([P, 1], F32)
            unused = prep.tile([P, TILES], F32)
            nc.scalar.activation(
                out=unused[:],
                in_=tiles["column_means"][:],
                func=ACT.Identity,
                accum_out=minus_shift[:],
            )
            tiles["minus_shift"] = minus_shift

        def exponents(head):
            tiles = heads[head]
            shifted = prep.tile([P, 2 * TILES], F32)
            nc.scalar.activation(
                out=shifted[:],
                in_=tiles["half_norms"][:],
                func=ACT.Identity,
                bias=tiles["minus_shift"][:, 0:1],
            )
            tiles["shifted"] = shifted
            tiles["key_bias"] = shifted[:, TILES : 2 * TILES]

        def query_factor(head):
            tiles = heads[head]
            q_factor = padded_factors[head % len(padded_factors)][:, 0:TILES]
            nc.scalar.activation(
                out=q_factor,
                in_=tiles["shifted"][:, 0:TILES],
                func=ACT.Exp,
                scale=-1.0,
            )
            tiles["q_factor"] = q_factor

        def key_term(head):
            tiles = heads[head]
            b = head // HEADS
            key_columns = tiles["half_norms"][:, TILES : 2 * TILES]
            nc.vector.tensor_tensor(
                out=key_columns,
                in0=mask_term[:, b * TILES : (b + 1) * TILES],
                in1=key_columns,
                op=ALU.subtract,
            )

        def turn(head, a):
            tiles = heads[head]
            turned_bank = turn_banks.tile([P, TILES, P], BF16, tag="turn")
            for j in range(TILES):
                nc.tensor.transpose(turned_bank[:, j, :], tiles["qk"][:, a, j, :], ident_bf16[:])
            tiles["turned_bank%d" % a] = turned_bank

        def turn_copy(head, a):
            tiles = heads[head]
            turned_sb = prep.tile([P, TILES, P], BF16, name="turned%d" % a)
            nc.scalar.copy(out=turned_sb[:], in_=tiles["turned_bank%d" % a][:])
            tiles["turned%d" % a] = turned_sb

        def v_group(head, c):
            tiles = heads[head]
            if c == 0:
                v_grouped = prep.tile([P, PASSES, FEATURES, PACK], BF16, align_bytes=64)
                tiles["v_grouped"] = v_grouped
            nc.vector.tensor_copy(
                out=tiles["v_grouped"][:, c].rearrange("p (g i) t -> p g t i", i=RUN),
                in_=tiles["v_rows"][:, c].rearrange("p t (g i) -> p g t i", i=RUN),
            )

        def v_quantize(head):
            tiles = heads[head]
            v_codes = prep.tile([P, PASSES, FEATURES], U32, align_bytes=64)
            v_scales = prep.tile([P, PASSES, FEATURES], U8, align_bytes=64)
            nc.vector.quantize_mx(
                out=v_codes[:].rearrange("p c w -> p (c w)").bitcast(FP8X4),
                scales=v_scales[:].rearrange("p c w -> p (c w)"),
                in_=tiles["v_grouped"][:].rearrange("p c w t -> p (c w t)"),
            )
            tiles["v_codes"] = v_codes
            tiles["v_scales"] = v_scales


        def scores_and_exp(step, tile_index):
            head, half = divmod(step, HALVES)
            tiles = heads[head]
            first = half * Q_TILES_PER_HALF
            c, t = divmod(tile_index, PACK)
            if t == 0:
                key_part = key_parts.tile([P, PACK, Q_HALF], F32)
                steps[step]["key_part%d" % c] = key_part
            score = score_banks.tile([P, Q_HALF], F32)
            nc.tensor.matmul(
                score[:],
                lhsT=tiles["turned1"][:, tile_index, :],
                rhs=tiles["turned0"][:, first : first + Q_TILES_PER_HALF, :].rearrange(
                    "d j p -> d (j p)"
                ),
                start=True,
                stop=True,
            )
            nc.scalar.activation(
                out=steps[step]["key_part%d" % c][:, t, :],
                in_=score[:],
                func=ACT.Exp,
                bias=tiles["key_bias"][:, tile_index : tile_index + 1],
            )

        def spread_factor(step):
            head, half = divmod(step, HALVES)
            first = half * Q_TILES_PER_HALF
            spread = factor_banks.tile([P, Q_HALF], F32)
            for i in range(Q_TILES_PER_HALF):
                nc.tensor.transpose(
                    spread[:, i * P : (i + 1) * P],
                    heads[head]["q_factor"][:, first + i : first + i + 1].to_broadcast([P, P]),
                    ident_f32[:],
                )
            steps[step]["spread"] = spread

        def factor_rows(head):
            turned_factors = turn_banks.tile([P, P], F32, tag="turn")
            nc.tensor.transpose(
                turned_factors[:], padded_factors[head % len(padded_factors)][:], ident_f32[:]
            )
            heads[head]["turned_factors"] = turned_factors

        def factor_spread(head):
            b, h = divmod(head, HEADS)
            rows = prep.tile([TILES, P], F32)
            nc.scalar.copy(out=rows[:], in_=heads[head]["turned_factors"][0:TILES, :])
            parked = out[b, h][0:TILES, :]
            nc.sync.dma_start(out=parked, in_=rows[:])
            for half in range(HALVES):
                first = half * Q_TILES_PER_HALF
                factors = work.tile([P, Q_HALF - Q_VECTOR], F32, name="factors%d" % half)
                nc.sync.dma_start(
                    out=factors[:],
                    in_=parked[first : first + Q_TILES_PER_HALF, :]
                    .rearrange("j p -> (j p)")[Q_VECTOR:Q_HALF]
                    .partition_broadcast(P),
                )
                heads[head]["factors%d" % half] = factors

        def factor_copy(step):
            factors = work.tile([P, Q_HALF - Q_VECTOR_FIRST], F32)
            nc.scalar.copy(out=factors[:], in_=steps[step]["spread"][:, Q_VECTOR_FIRST:Q_HALF])
            steps[step]["factors"] = factors

        def multiply(step, c):
            head, half = divmod(step, HALVES)
            tiles = steps[step]
            if c == 0:
                attn = single.tile([P, PASSES, Q_HALF, PACK], BF16, align_bytes=64)
                tiles["attn"] = attn
            attn = tiles["attn"]
            key_part = tiles["key_part%d" % c]
            if head < FIRST_HEADS:
                split = Q_VECTOR_FIRST
                factors = tiles["factors"][:]
            elif c == GPSIMD_PASS:
                split = Q_VECTOR if step < n_steps - LAST_STEPS else Q_VECTOR_LAST
                factors = heads[head]["factors%d" % half][:, split - Q_VECTOR :]
            else:
                split = Q_HALF
            if split < Q_HALF:
                nc.gpsimd.tensor_tensor(
                    out=attn[:, c, split:Q_HALF, :].rearrange("p (g i) t -> p g t i", i=RUN),
                    in0=key_part[:, :, split:Q_HALF].rearrange("p t (g i) -> p g t i", i=RUN),
                    in1=factors.rearrange("p (g i) -> p g i", i=RUN)
                    .unsqueeze(2)
                    .to_broadcast([P, (Q_HALF - split) // RUN, PACK, RUN]),
                    op=ALU.mult,
                )
            nc.vector.tensor_tensor(
                out=attn[:, c, 0:split, :].rearrange("p (g i) t -> p g t i", i=RUN),
                in0=key_part[:, :, 0:split].rearrange("p t (g i) -> p g t i", i=RUN),
                in1=tiles["spread"][:, 0:split]
                .rearrange("p (g i) -> p g i", i=RUN)
                .unsqueeze(2)
                .to_broadcast([P, split // RUN, PACK, RUN]),
                op=ALU.mult,
            )

        def quantize(step):
            tiles = steps[step]
            attn_codes = work.tile([P, PASSES, Q_HALF], U32, align_bytes=64)
            attn_scales = work.tile([P, PASSES, Q_HALF], U8, align_bytes=64)
            nc.vector.quantize_mx(
                out=attn_codes[:].rearrange("p c n -> p (c n)").bitcast(FP8X4),
                scales=attn_scales[:].rearrange("p c n -> p (c n)"),
                in_=tiles["attn"][:].rearrange("p c n t -> p (c n t)"),
            )
            tiles["attn_codes"] = attn_codes
            tiles["attn_scales"] = attn_scales

        def attn_times_v(step, first=0, n=Q_TILES_PER_HALF):
            head = step // HALVES
            tiles = steps[step]
            if first == 0:
                out_sums = out_banks.tile([P, n, FEATURES], F32, tag="out")
            else:
                out_sums = turn_banks.tile([P, n, FEATURES], F32, tag="turn")
            for i in range(n):
                queries = slice((first + i) * P, (first + i + 1) * P)
                for c in range(PASSES):
                    nc.tensor.matmul_mx(
                        out=out_sums[:, i, :],
                        lhsT=tiles["attn_codes"][:, c, queries].bitcast(FP8X4),
                        lhsT_scale=tiles["attn_scales"][:, c, queries],
                        rhs=heads[head]["v_codes"][:, c, :].bitcast(FP8X4),
                        rhs_scale=heads[head]["v_scales"][:, c, :],
                        start=(c == 0),
                        stop=(c == PASSES - 1),
                    )
            tiles["out_sums%d" % first] = out_sums

        def out_copy(step, copy, first=0, n=Q_TILES_PER_HALF):
            head, half = divmod(step, HALVES)
            if "out_rows" not in heads[head]:
                out_rows = prep.tile([P, TILES, FEATURES], F32)
                heads[head]["out_rows"] = out_rows
            start = half * Q_TILES_PER_HALF + first
            copy(
                out=heads[head]["out_rows"][:, start : start + n, :],
                in_=steps[step]["out_sums%d" % first][:],
            )

        def store(head, first, n):
            b, h = divmod(head, HEADS)
            nc.sync.dma_start(
                out=out[b, h].rearrange("(p j) f -> p j f", j=TILES)[:, first : first + n],
                in_=heads[head]["out_rows"][:, first : first + n],
            )

        ctx.enter_context(tc.manual_schedule())

        half_tiles = TILES // 2
        last_q = (half_tiles, half_tiles)
        last_k = (TILES + half_tiles, half_tiles)
        whole = (0, 2 * TILES)
        turn(0, 0)
        turn(0, 1)
        square_sums(0, range(half_tiles))
        norm_stats(0, *last_q)
        square_sums(0, range(TILES, TILES + half_tiles))
        norm_mean_part(0, *last_q)
        norm_stats(0, *last_k)
        norm_sum(0, *last_q)
        norm_mean_part(0, *last_k)
        turn_copy(0, 0)
        mean_over_partitions(0)
        mask_terms()
        norm_sum(0, *last_k)
        sum_shift(0)
        turn_copy(0, 1)
        key_term(0)
        exponents(0)
        query_factor(0)
        norm_stats(1, *whole)
        v_group(0, 0)
        v_group(0, 1)
        norm_mean_part(1, *whole)
        v_quantize(0)
        norm_sum(1, *whole)
        norm_stats(2, *whole)
        key_term(1)
        norm_mean_part(2, *whole)
        norm_stats(NORMS_AHEAD, 0, STATS_FIRST)
        norm_sum(2, *whole)
        key_term(2)

        chain = {}
        for head in range(1, n_heads):
            start = max((HALVES * head - 3) * TILES + 4, 3)
            stages = [
                (0, mean_over_partitions),
                (2, sum_shift),
                (3, exponents),
                (4, query_factor),
            ]
            if head >= FIRST_HEADS:
                stages += [(7, factor_rows), (9, factor_spread)]
            for offset, stage in stages:
                chain.setdefault(start + offset, []).append((stage, head))

        for step in range(n_steps):
            second = step % HALVES == 1
            head = step // HALVES
            next_head = head + 1
            norms_head = head + NORMS_AHEAD
            steps[step] = {}
            if not second and norms_head + 1 < n_heads:
                load(norms_head + 1)
            for tile_index in range(TILES):
                scores_and_exp(step, tile_index)
                for stage, chain_head in chain.get(step * TILES + tile_index, []):
                    stage(chain_head)
                if next_head < n_heads:
                    if tile_index == 2:
                        turn(next_head, 1 if second else 0)
                    if tile_index == 5:
                        turn_copy(next_head, 1 if second else 0)
                if tile_index == 1:
                    spread_factor(step)
                if tile_index == 4 and head < FIRST_HEADS:
                    factor_copy(step)
                if tile_index == 5 and step >= OUT_LAG:
                    attn_times_v(step - OUT_LAG)
                if tile_index == 7 and step >= OUT_LAG:
                    done = step - OUT_LAG
                    out_copy(done, nc.scalar.copy)
                    if done % HALVES == HALVES - 1:
                        store(done // HALVES, 0, TILES)
            multiply(step, 0)
            multiply(step, 1)
            if not second:
                if norms_head < n_heads:
                    norm_stats(norms_head, STATS_FIRST, 2 * TILES - STATS_FIRST)
                if next_head < n_heads:
                    v_group(next_head, 0)
            else:
                if norms_head + 1 < n_heads:
                    norm_stats(norms_head + 1, 0, STATS_FIRST)
                if next_head < n_heads:
                    v_group(next_head, 1)
                if norms_head < n_heads:
                    norm_sum(norms_head, *whole)
            quantize(step)
            if not second:
                if norms_head < n_heads:
                    norm_mean_part(norms_head, *whole)
            else:
                if next_head < n_heads:
                    v_quantize(next_head)
                if norms_head < n_heads:
                    key_term(norms_head)
        attn_times_v(n_steps - 2)
        out_copy(n_steps - 2, nc.scalar.copy)
        store(n_heads - 1, 0, Q_TILES_PER_HALF)
        pair = Q_TILES_PER_HALF // 2
        for first, copy in ((0, nc.scalar.copy), (pair, nc.vector.tensor_copy)):
            attn_times_v(n_steps - 1, first, pair)
            out_copy(n_steps - 1, copy, first, pair)
            store(n_heads - 1, Q_TILES_PER_HALF + first, pair)
